import numpy as np
import ml_dtypes


def mxq(x, axis, fmt="e4m3"):
    dtype, down = {"e4m3": (ml_dtypes.float8_e4m3fn, 7), "e5m2": (ml_dtypes.float8_e5m2, 14)}[fmt]
    v = np.moveaxis(np.asarray(x, np.float32).astype(ml_dtypes.bfloat16).astype(np.float64), axis, -1)
    blocks = v.reshape(v.shape[:-1] + (-1, 32))
    amax = np.abs(blocks).max(-1, keepdims=True)
    byte = np.maximum(np.where(amax > 0, np.frexp(amax)[1] - 1 + 127, 0) - down, 1)
    scale = np.exp2(byte - 127.0)
    codes = (blocks / scale).astype(np.float32).astype(dtype).astype(np.float64)
    return np.moveaxis((codes * scale).reshape(v.shape), -1, axis)


WIDE = False


def mx_kscale(k):
    if not WIDE:
        return np.ones(k)
    levels = np.array([10, -10, 5, -5, 0])
    a = np.random.permutation(np.resize(levels, k // 512 * 4)).reshape(k // 512, 4)
    idx = np.arange(k)
    return np.exp2(a[idx // 512, idx % 128 // 32])


BF16 = ml_dtypes.bfloat16


def bf(x):
    return np.asarray(x, np.float32).astype(BF16)


def f64(x):
    return np.asarray(x).astype(np.float64)


B, C, CQ, CV, H, W = 2, 1024, 128, 1024, 32, 64
P = H * W


def conv1x1(xq, w, b):
    y = (mxq(f64(w), 1, "e4m3") @ xq) + f64(b)[None, :, None]
    return y.reshape(B, w.shape[0], H, W)


def kronecker(y):
    return np.concatenate([y.mean(axis=3), y.mean(axis=2)], axis=2)


def setup_inputs():
    s = mx_kscale(C)
    g = 3.0 / np.sqrt(C)
    return {"x": bf(np.random.standard_normal((B, C, H, W)) * s[None, :, None, None]),
            "Wq": bf(np.random.standard_normal((CQ, C)) * g / s[None, :]),
            "bq": bf(np.random.standard_normal(CQ) * 0.1),
            "Wk": bf(np.random.standard_normal((CQ, C)) * g / s[None, :]),
            "bk": bf(np.random.standard_normal(CQ) * 0.1),
            "Wv": bf(np.random.standard_normal((CV, C)) * g / s[None, :]),
            "bv": bf(np.random.standard_normal(CV) * 0.1)}


def reference(x, Wq, bq, Wk, bk, Wv, bv):
    xq = mxq(f64(x).reshape(B, C, P), 1, "e4m3")
    q = kronecker(conv1x1(xq, Wq, bq))
    k = kronecker(conv1x1(xq, Wk, bk))
    v = kronecker(conv1x1(xq, Wv, bv))
    return q, k, v

@@ -1,0 +1,232 @@
+from contextlib import ExitStack
+
+import concourse.mybir as mybir
+from concourse.masks import make_identity
+
+F32 = mybir.dt.float32
+BF16 = mybir.dt.bfloat16
+U32 = mybir.dt.uint32
+U8 = mybir.dt.uint8
+FP8X4 = mybir.dt.float8_e4m3fn_x4
+ADD = mybir.AluOpType.add
+MULT = mybir.AluOpType.mult
+AXIS_X = mybir.AxisListType.X
+COPY = mybir.ActivationFunctionType.Copy
+
+P = 128
+PACK = 4
+K_PASS = P * PACK
+IMAGES, CHANNELS, HEIGHT, WIDTH = 2, 1024, 32, 64
+PASSES = CHANNELS // K_PASS
+O_TILES = 10
+CHUNK = 512
+CHUNK_ROWS = CHUNK // WIDTH
+IMAGE_CHUNKS = HEIGHT // CHUNK_ROWS
+N_CHUNKS = IMAGES * IMAGE_CHUNKS
+
+WEIGHTS_AHEAD = 2
+WEIGHT_LOADS_PER_X_LOAD = 4
+QUANTISE_AT_TILE = 7
+VECTOR_ROW_SUMS_EVERY = 5
+FINISH_TILES = 5
+
+FLOPS = 2 * O_TILES * P * CHANNELS * IMAGES * HEIGHT * WIDTH
+
+
+def tile_pam_module_pa_kernel(tc, x, Wq, bq, Wk, bk, Wv, bv, out_0, out_1, out_2):
+    nc = tc.nc
+
+    x_passes = x.rearrange("n (g p t) h w -> n g p t (h w)", g=PASSES, p=P, t=PACK)
+    weight_rows = [Wq, Wk] + [Wv[P * r : P * (r + 1), :] for r in range(O_TILES - 2)]
+    out_rows = [out_0, out_1] + [out_2[:, P * r : P * (r + 1), :] for r in range(O_TILES - 2)]
+
+    with ExitStack() as stack:
+        stack.enter_context(tc.manual_schedule())
+        const = stack.enter_context(tc.tile_pool(name="const", bufs=1))
+        x_raw_pool = stack.enter_context(tc.tile_pool(name="x_raw", bufs=N_CHUNKS))
+        w_raw_pool = stack.enter_context(tc.tile_pool(name="w_raw", bufs=O_TILES))
+        x_grouped_pool = stack.enter_context(tc.tile_pool(name="x_grouped", bufs=1))
+        w_grouped_pool = stack.enter_context(tc.tile_pool(name="w_grouped", bufs=2))
+        x_mx_pool = stack.enter_context(tc.tile_pool(name="x_mx", bufs=2))
+        unread_pool = stack.enter_context(tc.tile_pool(name="unread", bufs=4))
+        result_pool = stack.enter_context(tc.tile_pool(name="result", bufs=2))
+        banks = stack.enter_context(tc.psum_pool(name="banks", bufs=8))
+
+        identity = const.tile([P, P], F32)
+        make_identity(nc, identity[:])
+
+        x_raw_tiles = []
+        for c in range(N_CHUNKS):
+            x_raw = x_raw_pool.tile([P, PASSES, PACK, CHUNK], BF16)
+            x_raw_tiles.append(x_raw)
+        w_raw_tiles = []
+        for m in range(O_TILES):
+            w_raw = w_raw_pool.tile([P, CHANNELS], BF16)
+            w_raw_tiles.append(w_raw)
+
+        def load_x(c, g):
+            n, part = divmod(c, IMAGE_CHUNKS)
+            nc.sync.dma_start(
+                out=x_raw_tiles[c][:, g],
+                in_=x_passes[n, g][:, :, CHUNK * part : CHUNK * (part + 1)],
+            )
+
+        for g in range(PASSES):
+            load_x(0, g)
+        for m in range(O_TILES):
+            nc.sync.dma_start(out=w_raw_tiles[m][:], in_=weight_rows[m])
+            if (m + 1) % WEIGHT_LOADS_PER_X_LOAD == 0:
+                load_x(1, (m + 1) // WEIGHT_LOADS_PER_X_LOAD - 1)
+        for c in range(2, N_CHUNKS):
+            for g in range(PASSES):
+                load_x(c, g)
+
+        bias_rows = const.tile([P, P], BF16)
+        nc.vector.memset(bias_rows[:], 0.0)
+        nc.scalar.dma_start(out=bias_rows[0:1, :], in_=bq.rearrange("(r o) -> r o", r=1))
+        nc.scalar.dma_start(out=bias_rows[1:2, :], in_=bk.rearrange("(r o) -> r o", r=1))
+        nc.scalar.dma_start(
+            out=bias_rows[2:O_TILES, :], in_=bv.rearrange("(r o) -> r o", r=O_TILES - 2)
+        )
+
+        w_words = const.tile([P, O_TILES, PASSES * P], U32, align_bytes=64)
+        w_scales = const.tile([P, O_TILES, PASSES * P], U8, align_bytes=64)
+        bias = const.tile([P, O_TILES], F32)
+        row_sums = const.tile([P, IMAGES, O_TILES, HEIGHT], F32)
+        column_parts = const.tile([P, IMAGES, O_TILES, IMAGE_CHUNKS, WIDTH], F32)
+
+        def prepare_weights(m):
+            words = w_raw_tiles[m][:].bitcast(F32)
+            pairs = K_PASS // 2
+            transposed = banks.tile([P, PASSES * 2, P], F32, tag="bank")
+            for g in range(PASSES):
+                for u in range(2):
+                    nc.tensor.transpose(
+                        transposed[:, 2 * g + u, :],
+                        words[:, pairs * g + u : pairs * (g + 1) : 2],
+                        identity[:],
+                    )
+            w_grouped = w_grouped_pool.tile([P, PASSES * P * PACK], BF16, align_bytes=64)
+            nc.scalar.copy(
+                out=w_grouped[:].bitcast(F32).rearrange("p (g o u) -> p g o u", g=PASSES, u=2),
+                in_=transposed[:].rearrange("p (g u) o -> p g o u", u=2),
+            )
+            nc.vector.quantize_mx(
+                out=w_words[:, m, :].bitcast(FP8X4), scales=w_scales[:, m, :], in_=w_grouped[:]
+            )
+
+        def prepare_bias():
+            bias_rows_f32 = const.tile([P, P], F32)
+            nc.vector.tensor_copy(out=bias_rows_f32[:], in_=bias_rows[:])
+            bias_columns = banks.tile([P, P], F32, tag="bank")
+            nc.tensor.transpose(bias_columns[:], bias_rows_f32[:], identity[:])
+            nc.vector.tensor_copy(out=bias[:], in_=bias_columns[:, 0:O_TILES])
+
+        def quantise_x(x_grouped):
+            x_words = x_mx_pool.tile([P, PASSES * CHUNK], U32, align_bytes=64)
+            x_scales = x_mx_pool.tile([P, PASSES * CHUNK], U8, align_bytes=64)
+            nc.vector.quantize_mx(
+                out=x_words[:].bitcast(FP8X4),
+                scales=x_scales[:],
+                in_=x_grouped[:].rearrange("p g w t -> p (g w t)"),
+            )
+            return x_words, x_scales
+
+        def finish(n, first):
+            tiles = slice(first, first + FINISH_TILES)
+            column_sums = result_pool.tile([P, FINISH_TILES, WIDTH], F32)
+            nc.vector.tensor_reduce(
+                out=column_sums[:],
+                in_=column_parts[:, n, tiles].rearrange("p m c j -> p m j c"),
+                axis=AXIS_X,
+                op=ADD,
+            )
+            pooled = result_pool.tile([P, FINISH_TILES, HEIGHT + WIDTH], F32)
+            nc.vector.scalar_tensor_tensor(
+                out=pooled[:, :, 0:HEIGHT],
+                in0=row_sums[:, n, tiles],
+                scalar=1.0 / WIDTH,
+                in1=bias[:, tiles].unsqueeze(2).to_broadcast([P, FINISH_TILES, HEIGHT]),
+                op0=MULT,
+                op1=ADD,
+            )
+            nc.vector.scalar_tensor_tensor(
+                out=pooled[:, :, HEIGHT:],
+                in0=column_sums[:],
+                scalar=1.0 / HEIGHT,
+                in1=bias[:, tiles].unsqueeze(2).to_broadcast([P, FINISH_TILES, WIDTH]),
+                op0=MULT,
+                op1=ADD,
+            )
+            for k in range(FINISH_TILES):
+                nc.sync.dma_start(out=out_rows[first + k][n], in_=pooled[:, k, :])
+
+        x_grouped = x_grouped_pool.tile([P, PASSES, CHUNK, PACK], BF16, align_bytes=64)
+        for g in range(PASSES):
+            nc.vector.tensor_copy(
+                out=x_grouped[:, g], in_=x_raw_tiles[0][:, g].rearrange("p t w -> p w t")
+            )
+        x_words, x_scales = quantise_x(x_grouped)
+        for m in range(WEIGHTS_AHEAD):
+            prepare_weights(m)
+
+        for c in range(N_CHUNKS):
+            n, part = divmod(c, IMAGE_CHUNKS)
+            first_row = CHUNK_ROWS * part
+            if c + 1 < N_CHUNKS:
+                x_grouped = x_grouped_pool.tile([P, PASSES, CHUNK, PACK], BF16, align_bytes=64)
+                for g in range(PASSES):
+                    nc.gpsimd.tensor_scalar(
+                        out=x_grouped[:, g],
+                        in0=x_raw_tiles[c + 1][:, g].rearrange("p t w -> p w t"),
+                        scalar1=1.0,
+                        scalar2=0.0,
+                        op0=MULT,
+                        op1=ADD,
+                    )
+            for m in range(O_TILES):
+                if c == 0 and m + WEIGHTS_AHEAD < O_TILES:
+                    prepare_weights(m + WEIGHTS_AHEAD)
+                if m == QUANTISE_AT_TILE and c + 1 < N_CHUNKS:
+                    next_words, next_scales = quantise_x(x_grouped)
+
+                product = banks.tile([P, CHUNK], F32, tag="bank")
+                for g in range(PASSES):
+                    nc.tensor.matmul_mx(
+                        out=product[:],
+                        lhsT=w_words[:, m, P * g : P * (g + 1)].bitcast(FP8X4),
+                        lhsT_scale=w_scales[:, m, P * g : P * (g + 1)],
+                        rhs=x_words[:, CHUNK * g : CHUNK * (g + 1)].bitcast(FP8X4),
+                        rhs_scale=x_scales[:, CHUNK * g : CHUNK * (g + 1)],
+                        start=(g == 0),
+                        stop=(g == PASSES - 1),
+                    )
+
+                if m % VECTOR_ROW_SUMS_EVERY == VECTOR_ROW_SUMS_EVERY - 1:
+                    nc.vector.tensor_reduce(
+                        out=row_sums[:, n, m, first_row : first_row + CHUNK_ROWS],
+                        in_=product[:].rearrange("p (i j) -> p i j", j=WIDTH),
+                        axis=AXIS_X,
+                        op=ADD,
+                    )
+                else:
+                    unread = unread_pool.tile([P, CHUNK], F32)
+                    for i in range(CHUNK_ROWS):
+                        nc.scalar.activation(
+                            out=unread[:, WIDTH * i : WIDTH * (i + 1)],
+                            in_=product[:, WIDTH * i : WIDTH * (i + 1)],
+                            func=COPY,
+                            accum_out=row_sums[:, n, m, first_row + i : first_row + i + 1],
+                        )
+                nc.vector.tensor_reduce(
+                    out=column_parts[:, n, m, part, :],
+                    in_=product[:].rearrange("p (i j) -> p j i", j=WIDTH),
+                    axis=AXIS_X,
+                    op=ADD,
+                )
+                if part == IMAGE_CHUNKS - 1 and (m + 1) % FINISH_TILES == 0:
+                    finish(n, m + 1 - FINISH_TILES)
+            if c == 0:
+                prepare_bias()
+            if c + 1 < N_CHUNKS:
+                x_words, x_scales = next_words, next_scales

@@ -23,18 +23,24 @@ CHUNK = 512
 CHUNK_ROWS = CHUNK // WIDTH
 IMAGE_CHUNKS = HEIGHT // CHUNK_ROWS
 N_CHUNKS = IMAGES * IMAGE_CHUNKS
+HALVES = 2
+HALF_WIDTH = WIDTH // HALVES
+HALF_CHUNK = CHUNK // HALVES
+PSUM_BANKS = 8
+
+GROUP = 5
+READ_TWICE = 3
 
 WEIGHTS_AHEAD = 2
 WEIGHT_LOADS_PER_X_LOAD = 4
-QUANTISE_AT_TILE = 7
-VECTOR_ROW_SUMS_EVERY = 5
-FINISH_TILES = 5
+QUANTISE_AT_TILE = 5
 
 FLOPS = 2 * O_TILES * P * CHANNELS * IMAGES * HEIGHT * WIDTH
 
 
 def tile_pam_module_pa_kernel(tc, x, Wq, bq, Wk, bk, Wv, bv, out_0, out_1, out_2):
     nc = tc.nc
+    n_multiplied_twice = (GROUP - READ_TWICE) * (O_TILES // GROUP)
 
     x_passes = x.rearrange("n (g p t) h w -> n g p t (h w)", g=PASSES, p=P, t=PACK)
     weight_rows = [Wq, Wk] + [Wv[P * r : P * (r + 1), :] for r in range(O_TILES - 2)]
@@ -50,7 +56,12 @@ def tile_pam_module_pa_kernel(tc, x, Wq, bq, Wk, bk, Wv, bv, out_0, out_1, out_2
         x_mx_pool = stack.enter_context(tc.tile_pool(name="x_mx", bufs=2))
         unread_pool = stack.enter_context(tc.tile_pool(name="unread", bufs=4))
         result_pool = stack.enter_context(tc.tile_pool(name="result", bufs=2))
-        banks = stack.enter_context(tc.psum_pool(name="banks", bufs=8))
+        column_banks = stack.enter_context(
+            tc.psum_pool(name="column_banks", bufs=n_multiplied_twice)
+        )
+        banks = stack.enter_context(
+            tc.psum_pool(name="banks", bufs=PSUM_BANKS - n_multiplied_twice)
+        )
 
         identity = const.tile([P, P], F32)
         make_identity(nc, identity[:])
@@ -94,6 +105,7 @@ def tile_pam_module_pa_kernel(tc, x, Wq, bq, Wk, bk, Wv, bv, out_0, out_1, out_2
         bias = const.tile([P, O_TILES], F32)
         row_sums = const.tile([P, IMAGES, O_TILES, HEIGHT], F32)
         column_parts = const.tile([P, IMAGES, O_TILES, IMAGE_CHUNKS, WIDTH], F32)
+        column_sums = const.tile([P, IMAGES, O_TILES, WIDTH], F32)
 
         def prepare_weights(m):
             words = w_raw_tiles[m][:].bitcast(F32)
@@ -122,111 +134,169 @@ def tile_pam_module_pa_kernel(tc, x, Wq, bq, Wk, bk, Wv, bv, out_0, out_1, out_2
             nc.tensor.transpose(bias_columns[:], bias_rows_f32[:], identity[:])
             nc.vector.tensor_copy(out=bias[:], in_=bias_columns[:, 0:O_TILES])
 
-        def quantise_x(x_grouped):
-            x_words = x_mx_pool.tile([P, PASSES * CHUNK], U32, align_bytes=64)
-            x_scales = x_mx_pool.tile([P, PASSES * CHUNK], U8, align_bytes=64)
-            nc.vector.quantize_mx(
-                out=x_words[:].bitcast(FP8X4),
-                scales=x_scales[:],
-                in_=x_grouped[:].rearrange("p g w t -> p (g w t)"),
+        def regroup_x(engine, c):
+            x_grouped = x_grouped_pool.tile(
+                [P, PASSES, HALVES, HALF_CHUNK, PACK], BF16, align_bytes=64
             )
-            return x_words, x_scales
-
-        def finish(n, first):
-            tiles = slice(first, first + FINISH_TILES)
-            column_sums = result_pool.tile([P, FINISH_TILES, WIDTH], F32)
-            nc.vector.tensor_reduce(
-                out=column_sums[:],
-                in_=column_parts[:, n, tiles].rearrange("p m c j -> p m j c"),
-                axis=AXIS_X,
-                op=ADD,
-            )
-            pooled = result_pool.tile([P, FINISH_TILES, HEIGHT + WIDTH], F32)
-            nc.vector.scalar_tensor_tensor(
-                out=pooled[:, :, 0:HEIGHT],
-                in0=row_sums[:, n, tiles],
-                scalar=1.0 / WIDTH,
-                in1=bias[:, tiles].unsqueeze(2).to_broadcast([P, FINISH_TILES, HEIGHT]),
-                op0=MULT,
-                op1=ADD,
-            )
-            nc.vector.scalar_tensor_tensor(
-                out=pooled[:, :, HEIGHT:],
-                in0=column_sums[:],
-                scalar=1.0 / HEIGHT,
-                in1=bias[:, tiles].unsqueeze(2).to_broadcast([P, FINISH_TILES, WIDTH]),
-                op0=MULT,
-                op1=ADD,
-            )
-            for k in range(FINISH_TILES):
-                nc.sync.dma_start(out=out_rows[first + k][n], in_=pooled[:, k, :])
-
-        x_grouped = x_grouped_pool.tile([P, PASSES, CHUNK, PACK], BF16, align_bytes=64)
-        for g in range(PASSES):
-            nc.vector.tensor_copy(
-                out=x_grouped[:, g], in_=x_raw_tiles[0][:, g].rearrange("p t w -> p w t")
-            )
-        x_words, x_scales = quantise_x(x_grouped)
-        for m in range(WEIGHTS_AHEAD):
-            prepare_weights(m)
-
-        for c in range(N_CHUNKS):
-            n, part = divmod(c, IMAGE_CHUNKS)
-            first_row = CHUNK_ROWS * part
-            if c + 1 < N_CHUNKS:
-                x_grouped = x_grouped_pool.tile([P, PASSES, CHUNK, PACK], BF16, align_bytes=64)
-                for g in range(PASSES):
-                    nc.gpsimd.tensor_scalar(
-                        out=x_grouped[:, g],
-                        in0=x_raw_tiles[c + 1][:, g].rearrange("p t w -> p w t"),
+            for g in range(PASSES):
+                by_half = x_raw_tiles[c][:, g].rearrange(
+                    "p t (i h j) -> p h i j t", h=HALVES, j=HALF_WIDTH
+                )
+                for h in range(HALVES):
+                    engine.tensor_scalar(
+                        out=x_grouped[:, g, h].rearrange("p (i j) t -> p i j t", j=HALF_WIDTH),
+                        in0=by_half[:, h],
                         scalar1=1.0,
                         scalar2=0.0,
                         op0=MULT,
                         op1=ADD,
                     )
+            return x_grouped
+
+        def quantise_x(x_grouped):
+            x_words = x_mx_pool.tile([P, PASSES, CHUNK], U32, align_bytes=64)
+            x_scales = x_mx_pool.tile([P, PASSES, CHUNK], U8, align_bytes=64)
+            nc.vector.quantize_mx(
+                out=x_words[:].rearrange("p g w -> p (g w)").bitcast(FP8X4),
+                scales=x_scales[:].rearrange("p g w -> p (g w)"),
+                in_=x_grouped[:].rearrange("p g h w t -> p (g h w t)"),
+            )
+            return x_words, x_scales
+
+        def multiply(out, m, g, x_mx, columns, start, stop):
+            x_words, x_scales = x_mx
+            nc.tensor.matmul_mx(
+                out=out,
+                lhsT=w_words[:, m, P * g : P * (g + 1)].bitcast(FP8X4),
+                lhsT_scale=w_scales[:, m, P * g : P * (g + 1)],
+                rhs=x_words[:, g, columns].bitcast(FP8X4),
+                rhs_scale=x_scales[:, g, columns],
+                start=start,
+                stop=stop,
+            )
+
+        def sum_down_columns(out, bank):
+            nc.vector.tensor_reduce(
+                out=out.rearrange("p (h j) -> p h j", h=HALVES),
+                in_=bank.rearrange("p (h i j) -> p h j i", h=HALVES, j=HALF_WIDTH),
+                axis=AXIS_X,
+                op=ADD,
+            )
+
+        def read_twice_tile(n, part, m, x_mx):
+            product = banks.tile([P, CHUNK], F32, tag="bank")
+            for g in range(PASSES):
+                multiply(product[:], m, g, x_mx, slice(0, CHUNK), g == 0, g == PASSES - 1)
+            unread = unread_pool.tile([P, CHUNK], F32)
+            product_rows = product[:].rearrange("p (h i j) -> p i h j", h=HALVES, j=HALF_WIDTH)
+            unread_rows = unread[:].rearrange("p (h i j) -> p i h j", h=HALVES, j=HALF_WIDTH)
+            for i in range(CHUNK_ROWS):
+                row = CHUNK_ROWS * part + i
+                nc.scalar.activation(
+                    out=unread_rows[:, i],
+                    in_=product_rows[:, i],
+                    func=COPY,
+                    accum_out=row_sums[:, n, m, row : row + 1],
+                )
+            sum_down_columns(column_parts[:, n, m, part, :], product[:])
+
+        def multiplied_twice_tile(n, part, m, x_mx, column_bank):
+            row_part = banks.tile([P, HALF_CHUNK], F32, tag="bank")
+            for g in range(PASSES):
+                for h in range(HALVES):
+                    multiply(
+                        row_part[:],
+                        m,
+                        g,
+                        x_mx,
+                        slice(HALF_CHUNK * h, HALF_CHUNK * (h + 1)),
+                        g == 0 and h == 0,
+                        g == PASSES - 1 and h == HALVES - 1,
+                    )
+            nc.vector.tensor_reduce(
+                out=row_sums[:, n, m, CHUNK_ROWS * part : CHUNK_ROWS * (part + 1)],
+                in_=row_part[:].rearrange("p (i j) -> p i j", j=HALF_WIDTH),
+                axis=AXIS_X,
+                op=ADD,
+            )
+            for g in range(PASSES):
+                multiply(
+                    column_bank[:],
+                    m,
+                    g,
+                    x_mx,
+                    slice(0, CHUNK),
+                    part == 0 and g == 0,
+                    part == IMAGE_CHUNKS - 1 and g == PASSES - 1,
+                )
+            if part == IMAGE_CHUNKS - 1:
+                sum_down_columns(column_sums[:, n, m, :], column_bank[:])
+
+        def add_column_parts(n, first):
+            tiles = slice(first, first + READ_TWICE)
+            pair_sums = result_pool.tile([P, READ_TWICE, 2, WIDTH], F32)
+            nc.gpsimd.tensor_tensor(
+                out=pair_sums[:],
+                in0=column_parts[:, n, tiles, 0:2],
+                in1=column_parts[:, n, tiles, 2:4],
+                op=ADD,
+            )
+            nc.gpsimd.tensor_tensor(
+                out=column_sums[:, n, tiles],
+                in0=pair_sums[:, :, 0],
+                in1=pair_sums[:, :, 1],
+                op=ADD,
+            )
+
+        def finish(n, first):
+            group = slice(first, first + GROUP)
+            pooled = result_pool.tile([P, GROUP, HEIGHT + WIDTH], F32)
+            nc.vector.scalar_tensor_tensor(
+                out=pooled[:, :, 0:HEIGHT],
+                in0=row_sums[:, n, group],
+                scalar=1.0 / WIDTH,
+                in1=bias[:, group].unsqueeze(2).to_broadcast([P, GROUP, HEIGHT]),
+                op0=MULT,
+                op1=ADD,
+            )
+            nc.vector.scalar_tensor_tensor(
+                out=pooled[:, :, HEIGHT:],
+                in0=column_sums[:, n, group],
+                scalar=1.0 / HEIGHT,
+                in1=bias[:, group].unsqueeze(2).to_broadcast([P, GROUP, WIDTH]),
+                op0=MULT,
+                op1=ADD,
+            )
+            for k in range(GROUP):
+                nc.sync.dma_start(out=out_rows[first + k][n], in_=pooled[:, k, :])
+
+        x_mx = quantise_x(regroup_x(nc.vector, 0))
+        x_grouped = regroup_x(nc.gpsimd, 1)
+        for m in range(WEIGHTS_AHEAD):
+            prepare_weights(m)
+
+        column_bank_of = {}
+        for c in range(N_CHUNKS):
+            n, part = divmod(c, IMAGE_CHUNKS)
             for m in range(O_TILES):
                 if c == 0 and m + WEIGHTS_AHEAD < O_TILES:
                     prepare_weights(m + WEIGHTS_AHEAD)
                 if m == QUANTISE_AT_TILE and c + 1 < N_CHUNKS:
-                    next_words, next_scales = quantise_x(x_grouped)
-
-                product = banks.tile([P, CHUNK], F32, tag="bank")
-                for g in range(PASSES):
-                    nc.tensor.matmul_mx(
-                        out=product[:],
-                        lhsT=w_words[:, m, P * g : P * (g + 1)].bitcast(FP8X4),
-                        lhsT_scale=w_scales[:, m, P * g : P * (g + 1)],
-                        rhs=x_words[:, CHUNK * g : CHUNK * (g + 1)].bitcast(FP8X4),
-                        rhs_scale=x_scales[:, CHUNK * g : CHUNK * (g + 1)],
-                        start=(g == 0),
-                        stop=(g == PASSES - 1),
-                    )
-
-                if m % VECTOR_ROW_SUMS_EVERY == VECTOR_ROW_SUMS_EVERY - 1:
-                    nc.vector.tensor_reduce(
-                        out=row_sums[:, n, m, first_row : first_row + CHUNK_ROWS],
-                        in_=product[:].rearrange("p (i j) -> p i j", j=WIDTH),
-                        axis=AXIS_X,
-                        op=ADD,
-                    )
+                    next_x_mx = quantise_x(x_grouped)
+                    if c + 2 < N_CHUNKS:
+                        x_grouped = regroup_x(nc.gpsimd, c + 2)
+                if m % GROUP >= READ_TWICE:
+                    if part == 0:
+                        column_bank = column_banks.tile([P, CHUNK], F32)
+                        column_bank_of[m] = column_bank
+                    multiplied_twice_tile(n, part, m, x_mx, column_bank_of[m])
                 else:
-                    unread = unread_pool.tile([P, CHUNK], F32)
-                    for i in range(CHUNK_ROWS):
-                        nc.scalar.activation(
-                            out=unread[:, WIDTH * i : WIDTH * (i + 1)],
-                            in_=product[:, WIDTH * i : WIDTH * (i + 1)],
-                            func=COPY,
-                            accum_out=row_sums[:, n, m, first_row + i : first_row + i + 1],
-                        )
-                nc.vector.tensor_reduce(
-                    out=column_parts[:, n, m, part, :],
-                    in_=product[:].rearrange("p (i j) -> p j i", j=WIDTH),
-                    axis=AXIS_X,
-                    op=ADD,
-                )
-                if part == IMAGE_CHUNKS - 1 and (m + 1) % FINISH_TILES == 0:
-                    finish(n, m + 1 - FINISH_TILES)
+                    read_twice_tile(n, part, m, x_mx)
+                if part == IMAGE_CHUNKS - 1 and (m + 1) % GROUP == READ_TWICE:
+                    add_column_parts(n, m + 1 - READ_TWICE)
+                if part == IMAGE_CHUNKS - 1 and (m + 1) % GROUP == 0:
+                    finish(n, m + 1 - GROUP)
             if c == 0:
                 prepare_bias()
             if c + 1 < N_CHUNKS:
-                x_words, x_scales = next_words, next_scales
+                x_mx = next_x_mx

@@ -11,6 +11,7 @@ FP8X4 = mybir.dt.float8_e4m3fn_x4
 ADD = mybir.AluOpType.add
 MULT = mybir.AluOpType.mult
 AXIS_X = mybir.AxisListType.X
+AXIS_XY = mybir.AxisListType.XY
 COPY = mybir.ActivationFunctionType.Copy
 
 P = 128
@@ -29,7 +30,7 @@ HALF_CHUNK = CHUNK // HALVES
 PSUM_BANKS = 8
 
 GROUP = 5
-READ_TWICE = 3
+MULTIPLIED_TWICE = (2, 4, 6)
 
 WEIGHTS_AHEAD = 2
 WEIGHT_LOADS_PER_X_LOAD = 4
@@ -40,7 +41,7 @@ FLOPS = 2 * O_TILES * P * CHANNELS * IMAGES * HEIGHT * WIDTH
 
 def tile_pam_module_pa_kernel(tc, x, Wq, bq, Wk, bk, Wv, bv, out_0, out_1, out_2):
     nc = tc.nc
-    n_multiplied_twice = (GROUP - READ_TWICE) * (O_TILES // GROUP)
+    n_multiplied_twice = len(MULTIPLIED_TWICE)
 
     x_passes = x.rearrange("n (g p t) h w -> n g p t (h w)", g=PASSES, p=P, t=PACK)
     weight_rows = [Wq, Wk] + [Wv[P * r : P * (r + 1), :] for r in range(O_TILES - 2)]
@@ -104,8 +105,9 @@ def tile_pam_module_pa_kernel(tc, x, Wq, bq, Wk, bk, Wv, bv, out_0, out_1, out_2
         w_scales = const.tile([P, O_TILES, PASSES * P], U8, align_bytes=64)
         bias = const.tile([P, O_TILES], F32)
         row_sums = const.tile([P, IMAGES, O_TILES, HEIGHT], F32)
-        column_parts = const.tile([P, IMAGES, O_TILES, IMAGE_CHUNKS, WIDTH], F32)
-        column_sums = const.tile([P, IMAGES, O_TILES, WIDTH], F32)
+        column_parts = const.tile([P, IMAGES, IMAGE_CHUNKS, O_TILES, WIDTH], F32)
+        nc.vector.memset(column_parts[:], 0.0)
+        earlier_parts = const.tile([P, IMAGES, O_TILES, WIDTH], F32)
 
         def prepare_weights(m):
             words = w_raw_tiles[m][:].bitcast(F32)
@@ -187,18 +189,26 @@ def tile_pam_module_pa_kernel(tc, x, Wq, bq, Wk, bk, Wv, bv, out_0, out_1, out_2
             product = banks.tile([P, CHUNK], F32, tag="bank")
             for g in range(PASSES):
                 multiply(product[:], m, g, x_mx, slice(0, CHUNK), g == 0, g == PASSES - 1)
-            unread = unread_pool.tile([P, CHUNK], F32)
             product_rows = product[:].rearrange("p (h i j) -> p i h j", h=HALVES, j=HALF_WIDTH)
-            unread_rows = unread[:].rearrange("p (h i j) -> p i h j", h=HALVES, j=HALF_WIDTH)
-            for i in range(CHUNK_ROWS):
-                row = CHUNK_ROWS * part + i
-                nc.scalar.activation(
-                    out=unread_rows[:, i],
-                    in_=product_rows[:, i],
-                    func=COPY,
-                    accum_out=row_sums[:, n, m, row : row + 1],
+            first_row = CHUNK_ROWS * part
+            if m % 2 == 1:
+                unread = unread_pool.tile([P, CHUNK], F32)
+                unread_rows = unread[:].rearrange("p (h i j) -> p i h j", h=HALVES, j=HALF_WIDTH)
+                for i in range(CHUNK_ROWS):
+                    nc.scalar.activation(
+                        out=unread_rows[:, i],
+                        in_=product_rows[:, i],
+                        func=COPY,
+                        accum_out=row_sums[:, n, m, first_row + i : first_row + i + 1],
+                    )
+            else:
+                nc.vector.tensor_reduce(
+                    out=row_sums[:, n, m, first_row : first_row + CHUNK_ROWS],
+                    in_=product_rows,
+                    axis=AXIS_XY,
+                    op=ADD,
                 )
-            sum_down_columns(column_parts[:, n, m, part, :], product[:])
+            sum_down_columns(column_parts[:, n, part, m, :], product[:])
 
         def multiplied_twice_tile(n, part, m, x_mx, column_bank):
             row_part = banks.tile([P, HALF_CHUNK], F32, tag="bank")
@@ -230,26 +240,33 @@ def tile_pam_module_pa_kernel(tc, x, Wq, bq, Wk, bk, Wv, bv, out_0, out_1, out_2
                     part == IMAGE_CHUNKS - 1 and g == PASSES - 1,
                 )
             if part == IMAGE_CHUNKS - 1:
-                sum_down_columns(column_sums[:, n, m, :], column_bank[:])
+                sum_down_columns(column_parts[:, n, part, m, :], column_bank[:])
 
-        def add_column_parts(n, first):
-            tiles = slice(first, first + READ_TWICE)
-            pair_sums = result_pool.tile([P, READ_TWICE, 2, WIDTH], F32)
+        def add_earlier_parts(n, first):
+            group = slice(first, first + GROUP)
             nc.gpsimd.tensor_tensor(
-                out=pair_sums[:],
-                in0=column_parts[:, n, tiles, 0:2],
-                in1=column_parts[:, n, tiles, 2:4],
+                out=earlier_parts[:, n, group],
+                in0=column_parts[:, n, 0, group],
+                in1=column_parts[:, n, 1, group],
                 op=ADD,
             )
-            nc.gpsimd.tensor_tensor(
-                out=column_sums[:, n, tiles],
-                in0=pair_sums[:, :, 0],
-                in1=pair_sums[:, :, 1],
-                op=ADD,
-            )
+            for part in range(2, IMAGE_CHUNKS - 1):
+                nc.gpsimd.tensor_tensor(
+                    out=earlier_parts[:, n, group],
+                    in0=earlier_parts[:, n, group],
+                    in1=column_parts[:, n, part, group],
+                    op=ADD,
+                )
 
         def finish(n, first):
             group = slice(first, first + GROUP)
+            column_sums = result_pool.tile([P, GROUP, WIDTH], F32)
+            nc.vector.tensor_tensor(
+                out=column_sums[:],
+                in0=column_parts[:, n, IMAGE_CHUNKS - 1, group],
+                in1=earlier_parts[:, n, group],
+                op=ADD,
+            )
             pooled = result_pool.tile([P, GROUP, HEIGHT + WIDTH], F32)
             nc.vector.scalar_tensor_tensor(
                 out=pooled[:, :, 0:HEIGHT],
@@ -261,7 +278,7 @@ def tile_pam_module_pa_kernel(tc, x, Wq, bq, Wk, bk, Wv, bv, out_0, out_1, out_2
             )
             nc.vector.scalar_tensor_tensor(
                 out=pooled[:, :, HEIGHT:],
-                in0=column_sums[:, n, group],
+                in0=column_sums[:],
                 scalar=1.0 / HEIGHT,
                 in1=bias[:, group].unsqueeze(2).to_broadcast([P, GROUP, WIDTH]),
                 op0=MULT,
@@ -285,15 +302,15 @@ def tile_pam_module_pa_kernel(tc, x, Wq, bq, Wk, bk, Wv, bv, out_0, out_1, out_2
                     next_x_mx = quantise_x(x_grouped)
                     if c + 2 < N_CHUNKS:
                         x_grouped = regroup_x(nc.gpsimd, c + 2)
-                if m % GROUP >= READ_TWICE:
+                if m in MULTIPLIED_TWICE:
                     if part == 0:
                         column_bank = column_banks.tile([P, CHUNK], F32)
                         column_bank_of[m] = column_bank
                     multiplied_twice_tile(n, part, m, x_mx, column_bank_of[m])
                 else:
                     read_twice_tile(n, part, m, x_mx)
-                if part == IMAGE_CHUNKS - 1 and (m + 1) % GROUP == READ_TWICE:
-                    add_column_parts(n, m + 1 - READ_TWICE)
+                if part == IMAGE_CHUNKS - 2 and (m + 1) % GROUP == 0:
+                    add_earlier_parts(n, m + 1 - GROUP)
                 if part == IMAGE_CHUNKS - 1 and (m + 1) % GROUP == 0:
                     finish(n, m + 1 - GROUP)
             if c == 0:

@@ -11,7 +11,6 @@ FP8X4 = mybir.dt.float8_e4m3fn_x4
 ADD = mybir.AluOpType.add
 MULT = mybir.AluOpType.mult
 AXIS_X = mybir.AxisListType.X
-AXIS_XY = mybir.AxisListType.XY
 COPY = mybir.ActivationFunctionType.Copy
 
 P = 128
@@ -30,7 +29,7 @@ HALF_CHUNK = CHUNK // HALVES
 PSUM_BANKS = 8
 
 GROUP = 5
-MULTIPLIED_TWICE = (2, 4, 6)
+MULTIPLY_TWICE_EVERY = 3
 
 WEIGHTS_AHEAD = 2
 WEIGHT_LOADS_PER_X_LOAD = 4
@@ -41,7 +40,7 @@ FLOPS = 2 * O_TILES * P * CHANNELS * IMAGES * HEIGHT * WIDTH
 
 def tile_pam_module_pa_kernel(tc, x, Wq, bq, Wk, bk, Wv, bv, out_0, out_1, out_2):
     nc = tc.nc
-    n_multiplied_twice = len(MULTIPLIED_TWICE)
+    n_multiplied_twice = O_TILES // MULTIPLY_TWICE_EVERY
 
     x_passes = x.rearrange("n (g p t) h w -> n g p t (h w)", g=PASSES, p=P, t=PACK)
     weight_rows = [Wq, Wk] + [Wv[P * r : P * (r + 1), :] for r in range(O_TILES - 2)]
@@ -189,24 +188,16 @@ def tile_pam_module_pa_kernel(tc, x, Wq, bq, Wk, bk, Wv, bv, out_0, out_1, out_2
             product = banks.tile([P, CHUNK], F32, tag="bank")
             for g in range(PASSES):
                 multiply(product[:], m, g, x_mx, slice(0, CHUNK), g == 0, g == PASSES - 1)
+            unread = unread_pool.tile([P, CHUNK], F32)
             product_rows = product[:].rearrange("p (h i j) -> p i h j", h=HALVES, j=HALF_WIDTH)
-            first_row = CHUNK_ROWS * part
-            if m % 2 == 1:
-                unread = unread_pool.tile([P, CHUNK], F32)
-                unread_rows = unread[:].rearrange("p (h i j) -> p i h j", h=HALVES, j=HALF_WIDTH)
-                for i in range(CHUNK_ROWS):
-                    nc.scalar.activation(
-                        out=unread_rows[:, i],
-                        in_=product_rows[:, i],
-                        func=COPY,
-                        accum_out=row_sums[:, n, m, first_row + i : first_row + i + 1],
-                    )
-            else:
-                nc.vector.tensor_reduce(
-                    out=row_sums[:, n, m, first_row : first_row + CHUNK_ROWS],
-                    in_=product_rows,
-                    axis=AXIS_XY,
-                    op=ADD,
+            unread_rows = unread[:].rearrange("p (h i j) -> p i h j", h=HALVES, j=HALF_WIDTH)
+            for i in range(CHUNK_ROWS):
+                row = CHUNK_ROWS * part + i
+                nc.scalar.activation(
+                    out=unread_rows[:, i],
+                    in_=product_rows[:, i],
+                    func=COPY,
+                    accum_out=row_sums[:, n, m, row : row + 1],
                 )
             sum_down_columns(column_parts[:, n, part, m, :], product[:])
 
@@ -302,7 +293,7 @@ def tile_pam_module_pa_kernel(tc, x, Wq, bq, Wk, bk, Wv, bv, out_0, out_1, out_2
                     next_x_mx = quantise_x(x_grouped)
                     if c + 2 < N_CHUNKS:
                         x_grouped = regroup_x(nc.gpsimd, c + 2)
-                if m in MULTIPLIED_TWICE:
+                if m % MULTIPLY_TWICE_EVERY == MULTIPLY_TWICE_EVERY - 1:
                     if part == 0:
                         column_bank = column_banks.tile([P, CHUNK], F32)
                         column_bank_of[m] = column_bank

@@ -11,6 +11,7 @@ FP8X4 = mybir.dt.float8_e4m3fn_x4
 ADD = mybir.AluOpType.add
 MULT = mybir.AluOpType.mult
 AXIS_X = mybir.AxisListType.X
+AXIS_XY = mybir.AxisListType.XY
 COPY = mybir.ActivationFunctionType.Copy
 
 P = 128
@@ -30,6 +31,11 @@ PSUM_BANKS = 8
 
 GROUP = 5
 MULTIPLY_TWICE_EVERY = 3
+
+VECTOR_ROWS_TILE = 4
+VECTOR_ROWS_TILE_ODD = 9
+GPSIMD_COLUMNS_TILE = 0
+LAG = 4
 
 WEIGHTS_AHEAD = 2
 WEIGHT_LOADS_PER_X_LOAD = 4
@@ -51,10 +57,11 @@ def tile_pam_module_pa_kernel(tc, x, Wq, bq, Wk, bk, Wv, bv, out_0, out_1, out_2
         const = stack.enter_context(tc.tile_pool(name="const", bufs=1))
         x_raw_pool = stack.enter_context(tc.tile_pool(name="x_raw", bufs=N_CHUNKS))
         w_raw_pool = stack.enter_context(tc.tile_pool(name="w_raw", bufs=O_TILES))
-        x_grouped_pool = stack.enter_context(tc.tile_pool(name="x_grouped", bufs=1))
+        x_grouped_pool = stack.enter_context(tc.tile_pool(name="x_grouped", bufs=2))
         w_grouped_pool = stack.enter_context(tc.tile_pool(name="w_grouped", bufs=2))
         x_mx_pool = stack.enter_context(tc.tile_pool(name="x_mx", bufs=2))
-        unread_pool = stack.enter_context(tc.tile_pool(name="unread", bufs=4))
+        copy_pool = stack.enter_context(tc.tile_pool(name="copy", bufs=2 * LAG))
+        tree_pool = stack.enter_context(tc.tile_pool(name="tree", bufs=2))
         result_pool = stack.enter_context(tc.tile_pool(name="result", bufs=2))
         column_banks = stack.enter_context(
             tc.psum_pool(name="column_banks", bufs=n_multiplied_twice)
@@ -105,7 +112,17 @@ def tile_pam_module_pa_kernel(tc, x, Wq, bq, Wk, bk, Wv, bv, out_0, out_1, out_2
         bias = const.tile([P, O_TILES], F32)
         row_sums = const.tile([P, IMAGES, O_TILES, HEIGHT], F32)
         column_parts = const.tile([P, IMAGES, IMAGE_CHUNKS, O_TILES, WIDTH], F32)
-        nc.vector.memset(column_parts[:], 0.0)
+        for n in range(IMAGES):
+            nc.gpsimd.memset(
+                column_parts[
+                    :,
+                    n,
+                    0 : IMAGE_CHUNKS - 1,
+                    MULTIPLY_TWICE_EVERY - 1 : O_TILES : MULTIPLY_TWICE_EVERY,
+                    :,
+                ],
+                0.0,
+            )
         earlier_parts = const.tile([P, IMAGES, O_TILES, WIDTH], F32)
 
         def prepare_weights(m):
@@ -184,22 +201,55 @@ def tile_pam_module_pa_kernel(tc, x, Wq, bq, Wk, bk, Wv, bv, out_0, out_1, out_2
                 op=ADD,
             )
 
-        def read_twice_tile(n, part, m, x_mx):
+        def gpsimd_sum_down_columns(out, product_copy):
+            rows = product_copy.rearrange("p (h i j) -> p h i j", h=HALVES, j=HALF_WIDTH)
+            four = tree_pool.tile([P, HALVES, CHUNK_ROWS // 2, HALF_WIDTH], F32)
+            nc.gpsimd.tensor_tensor(
+                out=four[:], in0=rows[:, :, 0:4, :], in1=rows[:, :, 4:8, :], op=ADD
+            )
+            two = tree_pool.tile([P, HALVES, CHUNK_ROWS // 4, HALF_WIDTH], F32)
+            nc.gpsimd.tensor_tensor(
+                out=two[:], in0=four[:, :, 0:2, :], in1=four[:, :, 2:4, :], op=ADD
+            )
+            nc.gpsimd.tensor_tensor(
+                out=out.rearrange("p (h j) -> p h j", h=HALVES),
+                in0=two[:, :, 0, :],
+                in1=two[:, :, 1, :],
+                op=ADD,
+            )
+
+        def whole_product(m, x_mx):
             product = banks.tile([P, CHUNK], F32, tag="bank")
             for g in range(PASSES):
                 multiply(product[:], m, g, x_mx, slice(0, CHUNK), g == 0, g == PASSES - 1)
-            unread = unread_pool.tile([P, CHUNK], F32)
+            return product
+
+        def scalar_rows_tile(n, part, m, x_mx, vector_sums_columns):
+            product = whole_product(m, x_mx)
+            if vector_sums_columns:
+                sum_down_columns(column_parts[:, n, part, m, :], product[:])
+            product_copy = copy_pool.tile([P, CHUNK], F32)
             product_rows = product[:].rearrange("p (h i j) -> p i h j", h=HALVES, j=HALF_WIDTH)
-            unread_rows = unread[:].rearrange("p (h i j) -> p i h j", h=HALVES, j=HALF_WIDTH)
+            copy_rows = product_copy[:].rearrange("p (h i j) -> p i h j", h=HALVES, j=HALF_WIDTH)
             for i in range(CHUNK_ROWS):
                 row = CHUNK_ROWS * part + i
                 nc.scalar.activation(
-                    out=unread_rows[:, i],
+                    out=copy_rows[:, i],
                     in_=product_rows[:, i],
                     func=COPY,
                     accum_out=row_sums[:, n, m, row : row + 1],
                 )
+            return product_copy
+
+        def vector_tile(n, part, m, x_mx):
+            product = whole_product(m, x_mx)
             sum_down_columns(column_parts[:, n, part, m, :], product[:])
+            nc.vector.tensor_reduce(
+                out=row_sums[:, n, m, CHUNK_ROWS * part : CHUNK_ROWS * (part + 1)],
+                in_=product[:].rearrange("p (h i j) -> p i h j", h=HALVES, j=HALF_WIDTH),
+                axis=AXIS_XY,
+                op=ADD,
+            )
 
         def multiplied_twice_tile(n, part, m, x_mx, column_bank):
             row_part = banks.tile([P, HALF_CHUNK], F32, tag="bank")
@@ -284,9 +334,15 @@ def tile_pam_module_pa_kernel(tc, x, Wq, bq, Wk, bk, Wv, bv, out_0, out_1, out_2
             prepare_weights(m)
 
         column_bank_of = {}
+        waiting = []
+        n_done = 0
         for c in range(N_CHUNKS):
             n, part = divmod(c, IMAGE_CHUNKS)
             for m in range(O_TILES):
+                step = O_TILES * c + m
+                while n_done < len(waiting) and waiting[n_done][0] <= step:
+                    waiting[n_done][1](*waiting[n_done][2])
+                    n_done += 1
                 if c == 0 and m + WEIGHTS_AHEAD < O_TILES:
                     prepare_weights(m + WEIGHTS_AHEAD)
                 if m == QUANTISE_AT_TILE and c + 1 < N_CHUNKS:
@@ -298,13 +354,26 @@ def tile_pam_module_pa_kernel(tc, x, Wq, bq, Wk, bk, Wv, bv, out_0, out_1, out_2
                         column_bank = column_banks.tile([P, CHUNK], F32)
                         column_bank_of[m] = column_bank
                     multiplied_twice_tile(n, part, m, x_mx, column_bank_of[m])
+                elif m == VECTOR_ROWS_TILE or (m == VECTOR_ROWS_TILE_ODD and c % 2 == 1):
+                    vector_tile(n, part, m, x_mx)
                 else:
-                    read_twice_tile(n, part, m, x_mx)
+                    product_copy = scalar_rows_tile(n, part, m, x_mx, m != GPSIMD_COLUMNS_TILE)
+                    if m == GPSIMD_COLUMNS_TILE:
+                        waiting.append(
+                            (
+                                step + LAG,
+                                gpsimd_sum_down_columns,
+                                (column_parts[:, n, part, m, :], product_copy[:]),
+                            )
+                        )
                 if part == IMAGE_CHUNKS - 2 and (m + 1) % GROUP == 0:
-                    add_earlier_parts(n, m + 1 - GROUP)
+                    waiting.append((step + LAG, add_earlier_parts, (n, m + 1 - GROUP)))
                 if part == IMAGE_CHUNKS - 1 and (m + 1) % GROUP == 0:
-                    finish(n, m + 1 - GROUP)
+                    waiting.append((step + LAG, finish, (n, m + 1 - GROUP)))
             if c == 0:
                 prepare_bias()
             if c + 1 < N_CHUNKS:
                 x_mx = next_x_mx
+        while n_done < len(waiting):
+            waiting[n_done][1](*waiting[n_done][2])
+            n_done += 1

@@ -30,9 +30,9 @@ HALF_CHUNK = CHUNK // HALVES
 PSUM_BANKS = 8
 
 GROUP = 5
-MULTIPLY_TWICE_EVERY = 3
+MULTIPLIED_TWICE = (1, 5, 7)
 
-VECTOR_ROWS_TILE = 4
+VECTOR_ROWS_TILE = 3
 VECTOR_ROWS_TILE_ODD = 9
 GPSIMD_COLUMNS_TILE = 0
 LAG = 4
@@ -46,7 +46,7 @@ FLOPS = 2 * O_TILES * P * CHANNELS * IMAGES * HEIGHT * WIDTH
 
 def tile_pam_module_pa_kernel(tc, x, Wq, bq, Wk, bk, Wv, bv, out_0, out_1, out_2):
     nc = tc.nc
-    n_multiplied_twice = O_TILES // MULTIPLY_TWICE_EVERY
+    n_multiplied_twice = len(MULTIPLIED_TWICE)
 
     x_passes = x.rearrange("n (g p t) h w -> n g p t (h w)", g=PASSES, p=P, t=PACK)
     weight_rows = [Wq, Wk] + [Wv[P * r : P * (r + 1), :] for r in range(O_TILES - 2)]
@@ -57,7 +57,7 @@ def tile_pam_module_pa_kernel(tc, x, Wq, bq, Wk, bk, Wv, bv, out_0, out_1, out_2
         const = stack.enter_context(tc.tile_pool(name="const", bufs=1))
         x_raw_pool = stack.enter_context(tc.tile_pool(name="x_raw", bufs=N_CHUNKS))
         w_raw_pool = stack.enter_context(tc.tile_pool(name="w_raw", bufs=O_TILES))
-        x_grouped_pool = stack.enter_context(tc.tile_pool(name="x_grouped", bufs=2))
+        x_grouped_pool = stack.enter_context(tc.tile_pool(name="x_grouped", bufs=1))
         w_grouped_pool = stack.enter_context(tc.tile_pool(name="w_grouped", bufs=2))
         x_mx_pool = stack.enter_context(tc.tile_pool(name="x_mx", bufs=2))
         copy_pool = stack.enter_context(tc.tile_pool(name="copy", bufs=2 * LAG))
@@ -112,17 +112,8 @@ def tile_pam_module_pa_kernel(tc, x, Wq, bq, Wk, bk, Wv, bv, out_0, out_1, out_2
         bias = const.tile([P, O_TILES], F32)
         row_sums = const.tile([P, IMAGES, O_TILES, HEIGHT], F32)
         column_parts = const.tile([P, IMAGES, IMAGE_CHUNKS, O_TILES, WIDTH], F32)
-        for n in range(IMAGES):
-            nc.gpsimd.memset(
-                column_parts[
-                    :,
-                    n,
-                    0 : IMAGE_CHUNKS - 1,
-                    MULTIPLY_TWICE_EVERY - 1 : O_TILES : MULTIPLY_TWICE_EVERY,
-                    :,
-                ],
-                0.0,
-            )
+        for m in MULTIPLIED_TWICE:
+            nc.gpsimd.memset(column_parts[:, :, 0 : IMAGE_CHUNKS - 1, m, :], 0.0)
         earlier_parts = const.tile([P, IMAGES, O_TILES, WIDTH], F32)
 
         def prepare_weights(m):
@@ -349,7 +340,7 @@ def tile_pam_module_pa_kernel(tc, x, Wq, bq, Wk, bk, Wv, bv, out_0, out_1, out_2
                     next_x_mx = quantise_x(x_grouped)
                     if c + 2 < N_CHUNKS:
                         x_grouped = regroup_x(nc.gpsimd, c + 2)
-                if m % MULTIPLY_TWICE_EVERY == MULTIPLY_TWICE_EVERY - 1:
+                if m in MULTIPLIED_TWICE:
                     if part == 0:
                         column_bank = column_banks.tile([P, CHUNK], F32)
                         column_bank_of[m] = column_bank
@@ -357,15 +348,7 @@ def tile_pam_module_pa_kernel(tc, x, Wq, bq, Wk, bk, Wv, bv, out_0, out_1, out_2
                 elif m == VECTOR_ROWS_TILE or (m == VECTOR_ROWS_TILE_ODD and c % 2 == 1):
                     vector_tile(n, part, m, x_mx)
                 else:
-                    product_copy = scalar_rows_tile(n, part, m, x_mx, m != GPSIMD_COLUMNS_TILE)
-                    if m == GPSIMD_COLUMNS_TILE:
-                        waiting.append(
-                            (
-                                step + LAG,
-                                gpsimd_sum_down_columns,
-                                (column_parts[:, n, part, m, :], product_copy[:]),
-                            )
-                        )
+                    scalar_rows_tile(n, part, m, x_mx, True)
                 if part == IMAGE_CHUNKS - 2 and (m + 1) % GROUP == 0:
                     waiting.append((step + LAG, add_earlier_parts, (n, m + 1 - GROUP)))
                 if part == IMAGE_CHUNKS - 1 and (m + 1) % GROUP == 0:

@@ -40,6 +40,7 @@ LAG = 4
 WEIGHTS_AHEAD = 2
 WEIGHT_LOADS_PER_X_LOAD = 4
 QUANTISE_AT_TILE = 5
+SCALAR_REGROUPS_AT_TILE = 8
 
 FLOPS = 2 * O_TILES * P * CHANNELS * IMAGES * HEIGHT * WIDTH
 
@@ -143,23 +144,27 @@ def tile_pam_module_pa_kernel(tc, x, Wq, bq, Wk, bk, Wv, bv, out_0, out_1, out_2
             nc.tensor.transpose(bias_columns[:], bias_rows_f32[:], identity[:])
             nc.vector.tensor_copy(out=bias[:], in_=bias_columns[:, 0:O_TILES])
 
-        def regroup_x(engine, c):
+        def regroup_piece(engine, x_grouped, c, g, h):
+            out = x_grouped[:, g, h].rearrange("p (i j) t -> p i j t", j=HALF_WIDTH)
+            in_ = x_raw_tiles[c][:, g].rearrange(
+                "p t (i h j) -> p h i j t", h=HALVES, j=HALF_WIDTH
+            )[:, h]
+            if engine == "scalar":
+                nc.scalar.copy(out=out, in_=in_)
+            else:
+                compute = nc.vector if engine == "vector" else nc.gpsimd
+                compute.tensor_scalar(
+                    out=out, in0=in_, scalar1=1.0, scalar2=0.0, op0=MULT, op1=ADD
+                )
+
+        def regroup_x(engine, c, last_piece_too):
             x_grouped = x_grouped_pool.tile(
                 [P, PASSES, HALVES, HALF_CHUNK, PACK], BF16, align_bytes=64
             )
             for g in range(PASSES):
-                by_half = x_raw_tiles[c][:, g].rearrange(
-                    "p t (i h j) -> p h i j t", h=HALVES, j=HALF_WIDTH
-                )
                 for h in range(HALVES):
-                    engine.tensor_scalar(
-                        out=x_grouped[:, g, h].rearrange("p (i j) t -> p i j t", j=HALF_WIDTH),
-                        in0=by_half[:, h],
-                        scalar1=1.0,
-                        scalar2=0.0,
-                        op0=MULT,
-                        op1=ADD,
-                    )
+                    if last_piece_too or (g, h) != (PASSES - 1, HALVES - 1):
+                        regroup_piece(engine, x_grouped, c, g, h)
             return x_grouped
 
         def quantise_x(x_grouped):
@@ -319,8 +324,8 @@ def tile_pam_module_pa_kernel(tc, x, Wq, bq, Wk, bk, Wv, bv, out_0, out_1, out_2
             for k in range(GROUP):
                 nc.sync.dma_start(out=out_rows[first + k][n], in_=pooled[:, k, :])
 
-        x_mx = quantise_x(regroup_x(nc.vector, 0))
-        x_grouped = regroup_x(nc.gpsimd, 1)
+        x_mx = quantise_x(regroup_x("vector", 0, True))
+        x_grouped = regroup_x("gpsimd", 1, True)
         for m in range(WEIGHTS_AHEAD):
             prepare_weights(m)
 
@@ -339,7 +344,9 @@ def tile_pam_module_pa_kernel(tc, x, Wq, bq, Wk, bk, Wv, bv, out_0, out_1, out_2
                 if m == QUANTISE_AT_TILE and c + 1 < N_CHUNKS:
                     next_x_mx = quantise_x(x_grouped)
                     if c + 2 < N_CHUNKS:
-                        x_grouped = regroup_x(nc.gpsimd, c + 2)
+                        x_grouped = regroup_x("gpsimd", c + 2, False)
+                if m == SCALAR_REGROUPS_AT_TILE and c + 2 < N_CHUNKS:
+                    regroup_piece("scalar", x_grouped, c + 2, PASSES - 1, HALVES - 1)
                 if m in MULTIPLIED_TWICE:
                     if part == 0:
                         column_bank = column_banks.tile([P, CHUNK], F32)

@@ -34,6 +34,7 @@ MULTIPLIED_TWICE = (1, 5, 7)
 
 VECTOR_ROWS_TILE = 3
 VECTOR_ROWS_TILE_ODD = 9
+FIRST_SCALAR_ROWS_TILE_OF_CHUNK_0 = 8
 GPSIMD_COLUMNS_TILE = 0
 LAG = 4
 
@@ -70,6 +71,11 @@ def tile_pam_module_pa_kernel(tc, x, Wq, bq, Wk, bk, Wv, bv, out_0, out_1, out_2
         banks = stack.enter_context(
             tc.psum_pool(name="banks", bufs=PSUM_BANKS - n_multiplied_twice)
         )
+
+        warm_in = const.tile([P, 1], F32)
+        nc.vector.memset(warm_in[:], 0.0)
+        warm_out = const.tile([P, 1], F32)
+        nc.scalar.activation(out=warm_out[:], in_=warm_in[:], func=COPY)
 
         identity = const.tile([P, P], F32)
         make_identity(nc, identity[:])
@@ -151,9 +157,10 @@ def tile_pam_module_pa_kernel(tc, x, Wq, bq, Wk, bk, Wv, bv, out_0, out_1, out_2
             )[:, h]
             if engine == "scalar":
                 nc.scalar.copy(out=out, in_=in_)
+            elif engine == "vector":
+                nc.vector.tensor_copy(out=out, in_=in_)
             else:
-                compute = nc.vector if engine == "vector" else nc.gpsimd
-                compute.tensor_scalar(
+                nc.gpsimd.tensor_scalar(
                     out=out, in0=in_, scalar1=1.0, scalar2=0.0, op0=MULT, op1=ADD
                 )
 
@@ -167,9 +174,21 @@ def tile_pam_module_pa_kernel(tc, x, Wq, bq, Wk, bk, Wv, bv, out_0, out_1, out_2
                         regroup_piece(engine, x_grouped, c, g, h)
             return x_grouped
 
-        def quantise_x(x_grouped):
+        def new_x_mx():
             x_words = x_mx_pool.tile([P, PASSES, CHUNK], U32, align_bytes=64)
             x_scales = x_mx_pool.tile([P, PASSES, CHUNK], U8, align_bytes=64)
+            return x_words, x_scales
+
+        def quantise_x_pass(x_grouped, x_mx, g):
+            x_words, x_scales = x_mx
+            nc.vector.quantize_mx(
+                out=x_words[:, g, :].bitcast(FP8X4),
+                scales=x_scales[:, g, :],
+                in_=x_grouped[:, g].rearrange("p h w t -> p (h w t)"),
+            )
+
+        def quantise_x(x_grouped):
+            x_words, x_scales = new_x_mx()
             nc.vector.quantize_mx(
                 out=x_words[:].rearrange("p g w -> p (g w)").bitcast(FP8X4),
                 scales=x_scales[:].rearrange("p g w -> p (g w)"),
@@ -324,10 +343,13 @@ def tile_pam_module_pa_kernel(tc, x, Wq, bq, Wk, bk, Wv, bv, out_0, out_1, out_2
             for k in range(GROUP):
                 nc.sync.dma_start(out=out_rows[first + k][n], in_=pooled[:, k, :])
 
-        x_mx = quantise_x(regroup_x("vector", 0, True))
+        x_grouped = regroup_x("vector", 0, True)
+        x_mx = new_x_mx()
+        assert WEIGHTS_AHEAD == PASSES
+        for g in range(PASSES):
+            quantise_x_pass(x_grouped, x_mx, g)
+            prepare_weights(g)
         x_grouped = regroup_x("gpsimd", 1, True)
-        for m in range(WEIGHTS_AHEAD):
-            prepare_weights(m)
 
         column_bank_of = {}
         waiting = []
@@ -352,7 +374,11 @@ def tile_pam_module_pa_kernel(tc, x, Wq, bq, Wk, bk, Wv, bv, out_0, out_1, out_2
                         column_bank = column_banks.tile([P, CHUNK], F32)
                         column_bank_of[m] = column_bank
                     multiplied_twice_tile(n, part, m, x_mx, column_bank_of[m])
-                elif m == VECTOR_ROWS_TILE or (m == VECTOR_ROWS_TILE_ODD and c % 2 == 1):
+                elif (
+                    m == VECTOR_ROWS_TILE
+                    or (m == VECTOR_ROWS_TILE_ODD and c % 2 == 1)
+                    or (c == 0 and m < FIRST_SCALAR_ROWS_TILE_OF_CHUNK_0)
+                ):
                     vector_tile(n, part, m, x_mx)
                 else:
                     scalar_rows_tile(n, part, m, x_mx, True)

@@ -32,8 +32,7 @@ PSUM_BANKS = 8
 GROUP = 5
 MULTIPLIED_TWICE = (1, 5, 7)
 
-VECTOR_ROWS_TILE = 3
-VECTOR_ROWS_TILE_ODD = 9
+SCALAR_ROWS_TILES = (0, 2, 4, 6)
 FIRST_SCALAR_ROWS_TILE_OF_CHUNK_0 = 8
 GPSIMD_COLUMNS_TILE = 0
 LAG = 4
@@ -117,6 +116,7 @@ def tile_pam_module_pa_kernel(tc, x, Wq, bq, Wk, bk, Wv, bv, out_0, out_1, out_2
         w_words = const.tile([P, O_TILES, PASSES * P], U32, align_bytes=64)
         w_scales = const.tile([P, O_TILES, PASSES * P], U8, align_bytes=64)
         bias = const.tile([P, O_TILES], F32)
+        bias_wide = const.tile([P, O_TILES, WIDTH], F32)
         row_sums = const.tile([P, IMAGES, O_TILES, HEIGHT], F32)
         column_parts = const.tile([P, IMAGES, IMAGE_CHUNKS, O_TILES, WIDTH], F32)
         for m in MULTIPLIED_TWICE:
@@ -149,6 +149,14 @@ def tile_pam_module_pa_kernel(tc, x, Wq, bq, Wk, bk, Wv, bv, out_0, out_1, out_2
             bias_columns = banks.tile([P, P], F32, tag="bank")
             nc.tensor.transpose(bias_columns[:], bias_rows_f32[:], identity[:])
             nc.vector.tensor_copy(out=bias[:], in_=bias_columns[:, 0:O_TILES])
+            nc.gpsimd.tensor_scalar(
+                out=bias_wide[:],
+                in0=bias[:].unsqueeze(2).to_broadcast([P, O_TILES, WIDTH]),
+                scalar1=1.0,
+                scalar2=0.0,
+                op0=MULT,
+                op1=ADD,
+            )
 
         def regroup_piece(engine, x_grouped, c, g, h):
             out = x_grouped[:, g, h].rearrange("p (i j) t -> p i j t", j=HALF_WIDTH)
@@ -313,16 +321,23 @@ def tile_pam_module_pa_kernel(tc, x, Wq, bq, Wk, bk, Wv, bv, out_0, out_1, out_2
                     in1=column_parts[:, n, part, group],
                     op=ADD,
                 )
+            nc.gpsimd.tensor_scalar(
+                out=earlier_parts[:, n, group],
+                in0=earlier_parts[:, n, group],
+                scalar1=1.0 / HEIGHT,
+                scalar2=0.0,
+                op0=MULT,
+                op1=ADD,
+            )
+            nc.gpsimd.tensor_tensor(
+                out=earlier_parts[:, n, group],
+                in0=earlier_parts[:, n, group],
+                in1=bias_wide[:, group],
+                op=ADD,
+            )
 
         def finish(n, first):
             group = slice(first, first + GROUP)
-            column_sums = result_pool.tile([P, GROUP, WIDTH], F32)
-            nc.vector.tensor_tensor(
-                out=column_sums[:],
-                in0=column_parts[:, n, IMAGE_CHUNKS - 1, group],
-                in1=earlier_parts[:, n, group],
-                op=ADD,
-            )
             pooled = result_pool.tile([P, GROUP, HEIGHT + WIDTH], F32)
             nc.vector.scalar_tensor_tensor(
                 out=pooled[:, :, 0:HEIGHT],
@@ -334,9 +349,9 @@ def tile_pam_module_pa_kernel(tc, x, Wq, bq, Wk, bk, Wv, bv, out_0, out_1, out_2
             )
             nc.vector.scalar_tensor_tensor(
                 out=pooled[:, :, HEIGHT:],
-                in0=column_sums[:],
+                in0=column_parts[:, n, IMAGE_CHUNKS - 1, group],
                 scalar=1.0 / HEIGHT,
-                in1=bias[:, group].unsqueeze(2).to_broadcast([P, GROUP, WIDTH]),
+                in1=earlier_parts[:, n, group],
                 op0=MULT,
                 op1=ADD,
             )
@@ -374,14 +389,10 @@ def tile_pam_module_pa_kernel(tc, x, Wq, bq, Wk, bk, Wv, bv, out_0, out_1, out_2
                         column_bank = column_banks.tile([P, CHUNK], F32)
                         column_bank_of[m] = column_bank
                     multiplied_twice_tile(n, part, m, x_mx, column_bank_of[m])
-                elif (
-                    m == VECTOR_ROWS_TILE
-                    or (m == VECTOR_ROWS_TILE_ODD and c % 2 == 1)
-                    or (c == 0 and m < FIRST_SCALAR_ROWS_TILE_OF_CHUNK_0)
-                ):
-                    vector_tile(n, part, m, x_mx)
-                else:
+                elif c > 0 and m in SCALAR_ROWS_TILES:
                     scalar_rows_tile(n, part, m, x_mx, True)
+                else:
+                    vector_tile(n, part, m, x_mx)
                 if part == IMAGE_CHUNKS - 2 and (m + 1) % GROUP == 0:
                     waiting.append((step + LAG, add_earlier_parts, (n, m + 1 - GROUP)))
                 if part == IMAGE_CHUNKS - 1 and (m + 1) % GROUP == 0:

@@ -32,14 +32,15 @@ PSUM_BANKS = 8
 GROUP = 5
 MULTIPLIED_TWICE = (1, 5, 7)
 
-SCALAR_ROWS_TILES = (0, 2, 4, 6)
+SCALAR_ROWS_TILES = (0, 2, 4, 6, 8, 9)
+ALTERNATING_TILE = 9
 FIRST_SCALAR_ROWS_TILE_OF_CHUNK_0 = 8
 GPSIMD_COLUMNS_TILE = 0
 LAG = 4
 
 WEIGHTS_AHEAD = 2
 WEIGHT_LOADS_PER_X_LOAD = 4
-QUANTISE_AT_TILE = 5
+QUANTISE_AT_TILES = (5, 7)
 SCALAR_REGROUPS_AT_TILE = 8
 
 FLOPS = 2 * O_TILES * P * CHANNELS * IMAGES * HEIGHT * WIDTH
@@ -195,15 +196,6 @@ def tile_pam_module_pa_kernel(tc, x, Wq, bq, Wk, bk, Wv, bv, out_0, out_1, out_2
                 in_=x_grouped[:, g].rearrange("p h w t -> p (h w t)"),
             )
 
-        def quantise_x(x_grouped):
-            x_words, x_scales = new_x_mx()
-            nc.vector.quantize_mx(
-                out=x_words[:].rearrange("p g w -> p (g w)").bitcast(FP8X4),
-                scales=x_scales[:].rearrange("p g w -> p (g w)"),
-                in_=x_grouped[:].rearrange("p g h w t -> p (g h w t)"),
-            )
-            return x_words, x_scales
-
         def multiply(out, m, g, x_mx, columns, start, stop):
             x_words, x_scales = x_mx
             nc.tensor.matmul_mx(
@@ -355,8 +347,16 @@ def tile_pam_module_pa_kernel(tc, x, Wq, bq, Wk, bk, Wv, bv, out_0, out_1, out_2
                 op0=MULT,
                 op1=ADD,
             )
-            for k in range(GROUP):
+            n_alone = max(0, 2 - first)
+            for k in range(n_alone):
                 nc.sync.dma_start(out=out_rows[first + k][n], in_=pooled[:, k, :])
+            v_first = first + n_alone - 2
+            nc.sync.dma_start(
+                out=out_2[n, P * v_first : P * (first + GROUP - 2), :].rearrange(
+                    "(k p) f -> p k f", p=P
+                ),
+                in_=pooled[:, n_alone:GROUP, :],
+            )
 
         x_grouped = regroup_x("vector", 0, True)
         x_mx = new_x_mx()
@@ -378,9 +378,12 @@ def tile_pam_module_pa_kernel(tc, x, Wq, bq, Wk, bk, Wv, bv, out_0, out_1, out_2
                     n_done += 1
                 if c == 0 and m + WEIGHTS_AHEAD < O_TILES:
                     prepare_weights(m + WEIGHTS_AHEAD)
-                if m == QUANTISE_AT_TILE and c + 1 < N_CHUNKS:
-                    next_x_mx = quantise_x(x_grouped)
-                    if c + 2 < N_CHUNKS:
+                if m in QUANTISE_AT_TILES and c + 1 < N_CHUNKS:
+                    g = QUANTISE_AT_TILES.index(m)
+                    if g == 0:
+                        next_x_mx = new_x_mx()
+                    quantise_x_pass(x_grouped, next_x_mx, g)
+                    if g == PASSES - 1 and c + 2 < N_CHUNKS:
                         x_grouped = regroup_x("gpsimd", c + 2, False)
                 if m == SCALAR_REGROUPS_AT_TILE and c + 2 < N_CHUNKS:
                     regroup_piece("scalar", x_grouped, c + 2, PASSES - 1, HALVES - 1)
@@ -389,10 +392,14 @@ def tile_pam_module_pa_kernel(tc, x, Wq, bq, Wk, bk, Wv, bv, out_0, out_1, out_2
                         column_bank = column_banks.tile([P, CHUNK], F32)
                         column_bank_of[m] = column_bank
                     multiplied_twice_tile(n, part, m, x_mx, column_bank_of[m])
-                elif c > 0 and m in SCALAR_ROWS_TILES:
-                    scalar_rows_tile(n, part, m, x_mx, True)
-                else:
+                elif (
+                    m not in SCALAR_ROWS_TILES
+                    or (m == ALTERNATING_TILE and c % 2 == 1)
+                    or (c == 0 and m < FIRST_SCALAR_ROWS_TILE_OF_CHUNK_0)
+                ):
                     vector_tile(n, part, m, x_mx)
+                else:
+                    scalar_rows_tile(n, part, m, x_mx, True)
                 if part == IMAGE_CHUNKS - 2 and (m + 1) % GROUP == 0:
                     waiting.append((step + LAG, add_earlier_parts, (n, m + 1 - GROUP)))
                 if part == IMAGE_CHUNKS - 1 and (m + 1) % GROUP == 0:

@@ -43,6 +43,9 @@ WEIGHT_LOADS_PER_X_LOAD = 4
 QUANTISE_AT_TILES = (5, 7)
 SCALAR_REGROUPS_AT_TILE = 8
 
+WARM_MATMULS_BEFORE_LOADS_LAND = 12
+WARM_MATMULS_AFTER_A_WEIGHT_TILE = 2
+
 FLOPS = 2 * O_TILES * P * CHANNELS * IMAGES * HEIGHT * WIDTH
 
 
@@ -76,6 +79,18 @@ def tile_pam_module_pa_kernel(tc, x, Wq, bq, Wk, bk, Wv, bv, out_0, out_1, out_2
         nc.vector.memset(warm_in[:], 0.0)
         warm_out = const.tile([P, 1], F32)
         nc.scalar.activation(out=warm_out[:], in_=warm_in[:], func=COPY)
+
+        warm_operand = const.tile([P, CHUNK], BF16)
+        nc.gpsimd.memset(warm_operand[:], 0.0)
+        warm_bank = banks.tile([P, CHUNK], F32, tag="bank")
+
+        def warm_tensor_engine(n_matmuls):
+            for k in range(n_matmuls):
+                nc.tensor.matmul(
+                    warm_bank[:], lhsT=warm_operand[:, 0:P], rhs=warm_operand[:], start=True, stop=True
+                )
+
+        warm_tensor_engine(WARM_MATMULS_BEFORE_LOADS_LAND)
 
         identity = const.tile([P, P], F32)
         make_identity(nc, identity[:])
@@ -364,6 +379,7 @@ def tile_pam_module_pa_kernel(tc, x, Wq, bq, Wk, bk, Wv, bv, out_0, out_1, out_2
         for g in range(PASSES):
             quantise_x_pass(x_grouped, x_mx, g)
             prepare_weights(g)
+            warm_tensor_engine(WARM_MATMULS_AFTER_A_WEIGHT_TILE)
         x_grouped = regroup_x("gpsimd", 1, True)
 
         column_bank_of = {}

@@ -41,7 +41,7 @@ LAG = 4
 WEIGHTS_AHEAD = 2
 WEIGHT_LOADS_PER_X_LOAD = 4
 QUANTISE_AT_TILES = (5, 7)
-SCALAR_REGROUPS_AT_TILE = 8
+SCALAR_REGROUPS_AT_TILES = (8, 0, 2, 4)
 
 WARM_MATMULS_BEFORE_LOADS_LAND = 12
 WARM_MATMULS_AFTER_A_WEIGHT_TILE = 2
@@ -174,11 +174,11 @@ def tile_pam_module_pa_kernel(tc, x, Wq, bq, Wk, bk, Wv, bv, out_0, out_1, out_2
                 op1=ADD,
             )
 
-        def regroup_piece(engine, x_grouped, c, g, h):
-            out = x_grouped[:, g, h].rearrange("p (i j) t -> p i j t", j=HALF_WIDTH)
+        def regroup_piece(engine, x_grouped, c, g, h, rows=slice(0, CHUNK_ROWS)):
+            out = x_grouped[:, g, h].rearrange("p (i j) t -> p i j t", j=HALF_WIDTH)[:, rows]
             in_ = x_raw_tiles[c][:, g].rearrange(
                 "p t (i h j) -> p h i j t", h=HALVES, j=HALF_WIDTH
-            )[:, h]
+            )[:, h, rows]
             if engine == "scalar":
                 nc.scalar.copy(out=out, in_=in_)
             elif engine == "vector":
@@ -401,8 +401,19 @@ def tile_pam_module_pa_kernel(tc, x, Wq, bq, Wk, bk, Wv, bv, out_0, out_1, out_2
                     quantise_x_pass(x_grouped, next_x_mx, g)
                     if g == PASSES - 1 and c + 2 < N_CHUNKS:
                         x_grouped = regroup_x("gpsimd", c + 2, False)
-                if m == SCALAR_REGROUPS_AT_TILE and c + 2 < N_CHUNKS:
-                    regroup_piece("scalar", x_grouped, c + 2, PASSES - 1, HALVES - 1)
+                if m in SCALAR_REGROUPS_AT_TILES:
+                    k = SCALAR_REGROUPS_AT_TILES.index(m)
+                    chunk = c + 2 if k == 0 else c + 1
+                    if 2 <= chunk < N_CHUNKS:
+                        share = CHUNK_ROWS // len(SCALAR_REGROUPS_AT_TILES)
+                        regroup_piece(
+                            "scalar",
+                            x_grouped,
+                            chunk,
+                            PASSES - 1,
+                            HALVES - 1,
+                            slice(share * k, share * (k + 1)),
+                        )
                 if m in MULTIPLIED_TWICE:
                     if part == 0:
                         column_bank = column_banks.tile([P, CHUNK], F32)

@@ -43,7 +43,8 @@ WEIGHT_LOADS_PER_X_LOAD = 4
 QUANTISE_AT_TILES = (5, 7)
 SCALAR_REGROUPS_AT_TILES = (8, 0, 2, 4)
 
-WARM_MATMULS_BEFORE_LOADS_LAND = 12
+WARM_MATMULS_BEFORE_LOADS_LAND = 9
+BIAS_TRANSPOSED_AT_TILE_OF_CHUNK_1 = 4
 WARM_MATMULS_AFTER_A_WEIGHT_TILE = 2
 
 FLOPS = 2 * O_TILES * P * CHANNELS * IMAGES * HEIGHT * WIDTH
@@ -159,9 +160,12 @@ def tile_pam_module_pa_kernel(tc, x, Wq, bq, Wk, bk, Wv, bv, out_0, out_1, out_2
                 out=w_words[:, m, :].bitcast(FP8X4), scales=w_scales[:, m, :], in_=w_grouped[:]
             )
 
-        def prepare_bias():
-            bias_rows_f32 = const.tile([P, P], F32)
+        bias_rows_f32 = const.tile([P, P], F32)
+
+        def cast_bias():
             nc.vector.tensor_copy(out=bias_rows_f32[:], in_=bias_rows[:])
+
+        def transpose_bias():
             bias_columns = banks.tile([P, P], F32, tag="bank")
             nc.tensor.transpose(bias_columns[:], bias_rows_f32[:], identity[:])
             nc.vector.tensor_copy(out=bias[:], in_=bias_columns[:, 0:O_TILES])
@@ -346,22 +350,42 @@ def tile_pam_module_pa_kernel(tc, x, Wq, bq, Wk, bk, Wv, bv, out_0, out_1, out_2
         def finish(n, first):
             group = slice(first, first + GROUP)
             pooled = result_pool.tile([P, GROUP, HEIGHT + WIDTH], F32)
-            nc.vector.scalar_tensor_tensor(
-                out=pooled[:, :, 0:HEIGHT],
-                in0=row_sums[:, n, group],
-                scalar=1.0 / WIDTH,
-                in1=bias[:, group].unsqueeze(2).to_broadcast([P, GROUP, HEIGHT]),
-                op0=MULT,
-                op1=ADD,
-            )
-            nc.vector.scalar_tensor_tensor(
-                out=pooled[:, :, HEIGHT:],
-                in0=column_parts[:, n, IMAGE_CHUNKS - 1, group],
-                scalar=1.0 / HEIGHT,
-                in1=earlier_parts[:, n, group],
-                op0=MULT,
-                op1=ADD,
-            )
+            if (n, first) == (IMAGES - 1, 0):
+                for out, in0, factor, in1 in (
+                    (
+                        pooled[:, :, 0:HEIGHT],
+                        row_sums[:, n, group],
+                        1.0 / WIDTH,
+                        bias_wide[:, group, 0:HEIGHT],
+                    ),
+                    (
+                        pooled[:, :, HEIGHT:],
+                        column_parts[:, n, IMAGE_CHUNKS - 1, group],
+                        1.0 / HEIGHT,
+                        earlier_parts[:, n, group],
+                    ),
+                ):
+                    nc.gpsimd.tensor_scalar(
+                        out=out, in0=in0, scalar1=factor, scalar2=0.0, op0=MULT, op1=ADD
+                    )
+                    nc.gpsimd.tensor_tensor(out=out, in0=out, in1=in1, op=ADD)
+            else:
+                nc.vector.scalar_tensor_tensor(
+                    out=pooled[:, :, 0:HEIGHT],
+                    in0=row_sums[:, n, group],
+                    scalar=1.0 / WIDTH,
+                    in1=bias[:, group].unsqueeze(2).to_broadcast([P, GROUP, HEIGHT]),
+                    op0=MULT,
+                    op1=ADD,
+                )
+                nc.vector.scalar_tensor_tensor(
+                    out=pooled[:, :, HEIGHT:],
+                    in0=column_parts[:, n, IMAGE_CHUNKS - 1, group],
+                    scalar=1.0 / HEIGHT,
+                    in1=earlier_parts[:, n, group],
+                    op0=MULT,
+                    op1=ADD,
+                )
             n_alone = max(0, 2 - first)
             for k in range(n_alone):
                 nc.sync.dma_start(out=out_rows[first + k][n], in_=pooled[:, k, :])
@@ -394,6 +418,8 @@ def tile_pam_module_pa_kernel(tc, x, Wq, bq, Wk, bk, Wv, bv, out_0, out_1, out_2
                     n_done += 1
                 if c == 0 and m + WEIGHTS_AHEAD < O_TILES:
                     prepare_weights(m + WEIGHTS_AHEAD)
+                if (c, m) == (1, BIAS_TRANSPOSED_AT_TILE_OF_CHUNK_1):
+                    transpose_bias()
                 if m in QUANTISE_AT_TILES and c + 1 < N_CHUNKS:
                     g = QUANTISE_AT_TILES.index(m)
                     if g == 0:
@@ -432,7 +458,7 @@ def tile_pam_module_pa_kernel(tc, x, Wq, bq, Wk, bk, Wv, bv, out_0, out_1, out_2
                 if part == IMAGE_CHUNKS - 1 and (m + 1) % GROUP == 0:
                     waiting.append((step + LAG, finish, (n, m + 1 - GROUP)))
             if c == 0:
-                prepare_bias()
+                cast_bias()
             if c + 1 < N_CHUNKS:
                 x_mx = next_x_mx
         while n_done < len(waiting):

@@ -34,18 +34,18 @@ MULTIPLIED_TWICE = (1, 5, 7)
 
 SCALAR_ROWS_TILES = (0, 2, 4, 6, 8, 9)
 ALTERNATING_TILE = 9
-FIRST_SCALAR_ROWS_TILE_OF_CHUNK_0 = 8
+FIRST_SCALAR_ROWS_TILE_OF_CHUNK_0 = 2
 GPSIMD_COLUMNS_TILE = 0
 LAG = 4
 
 WEIGHTS_AHEAD = 2
-WEIGHT_LOADS_PER_X_LOAD = 4
+X_LOADS_FOLLOW_WEIGHT_TILES = (5, 9)
 QUANTISE_AT_TILES = (5, 7)
 SCALAR_REGROUPS_AT_TILES = (8, 0, 2, 4)
 
 WARM_MATMULS_BEFORE_LOADS_LAND = 9
 BIAS_TRANSPOSED_AT_TILE_OF_CHUNK_1 = 4
-WARM_MATMULS_AFTER_A_WEIGHT_TILE = 2
+TRANSPOSES_AHEAD = 4
 
 FLOPS = 2 * O_TILES * P * CHANNELS * IMAGES * HEIGHT * WIDTH
 
@@ -64,7 +64,7 @@ def tile_pam_module_pa_kernel(tc, x, Wq, bq, Wk, bk, Wv, bv, out_0, out_1, out_2
         x_raw_pool = stack.enter_context(tc.tile_pool(name="x_raw", bufs=N_CHUNKS))
         w_raw_pool = stack.enter_context(tc.tile_pool(name="w_raw", bufs=O_TILES))
         x_grouped_pool = stack.enter_context(tc.tile_pool(name="x_grouped", bufs=1))
-        w_grouped_pool = stack.enter_context(tc.tile_pool(name="w_grouped", bufs=2))
+        w_grouped_pool = stack.enter_context(tc.tile_pool(name="w_grouped", bufs=TRANSPOSES_AHEAD))
         x_mx_pool = stack.enter_context(tc.tile_pool(name="x_mx", bufs=2))
         copy_pool = stack.enter_context(tc.tile_pool(name="copy", bufs=2 * LAG))
         tree_pool = stack.enter_context(tc.tile_pool(name="tree", bufs=2))
@@ -116,8 +116,8 @@ def tile_pam_module_pa_kernel(tc, x, Wq, bq, Wk, bk, Wv, bv, out_0, out_1, out_2
             load_x(0, g)
         for m in range(O_TILES):
             nc.sync.dma_start(out=w_raw_tiles[m][:], in_=weight_rows[m])
-            if (m + 1) % WEIGHT_LOADS_PER_X_LOAD == 0:
-                load_x(1, (m + 1) // WEIGHT_LOADS_PER_X_LOAD - 1)
+            if m in X_LOADS_FOLLOW_WEIGHT_TILES:
+                load_x(1, X_LOADS_FOLLOW_WEIGHT_TILES.index(m))
         for c in range(2, N_CHUNKS):
             for g in range(PASSES):
                 load_x(c, g)
@@ -140,7 +140,9 @@ def tile_pam_module_pa_kernel(tc, x, Wq, bq, Wk, bk, Wv, bv, out_0, out_1, out_2
             nc.gpsimd.memset(column_parts[:, :, 0 : IMAGE_CHUNKS - 1, m, :], 0.0)
         earlier_parts = const.tile([P, IMAGES, O_TILES, WIDTH], F32)
 
-        def prepare_weights(m):
+        w_grouped_of = {}
+
+        def transpose_weights(m):
             words = w_raw_tiles[m][:].bitcast(F32)
             pairs = K_PASS // 2
             transposed = banks.tile([P, PASSES * 2, P], F32, tag="bank")
@@ -156,8 +158,13 @@ def tile_pam_module_pa_kernel(tc, x, Wq, bq, Wk, bk, Wv, bv, out_0, out_1, out_2
                 out=w_grouped[:].bitcast(F32).rearrange("p (g o u) -> p g o u", g=PASSES, u=2),
                 in_=transposed[:].rearrange("p (g u) o -> p g o u", u=2),
             )
+            w_grouped_of[m] = w_grouped
+
+        def quantise_weights(m):
             nc.vector.quantize_mx(
-                out=w_words[:, m, :].bitcast(FP8X4), scales=w_scales[:, m, :], in_=w_grouped[:]
+                out=w_words[:, m, :].bitcast(FP8X4),
+                scales=w_scales[:, m, :],
+                in_=w_grouped_of[m][:],
             )
 
         bias_rows_f32 = const.tile([P, P], F32)
@@ -400,10 +407,11 @@ def tile_pam_module_pa_kernel(tc, x, Wq, bq, Wk, bk, Wv, bv, out_0, out_1, out_2
         x_grouped = regroup_x("vector", 0, True)
         x_mx = new_x_mx()
         assert WEIGHTS_AHEAD == PASSES
+        for m in range(TRANSPOSES_AHEAD):
+            transpose_weights(m)
         for g in range(PASSES):
             quantise_x_pass(x_grouped, x_mx, g)
-            prepare_weights(g)
-            warm_tensor_engine(WARM_MATMULS_AFTER_A_WEIGHT_TILE)
+            quantise_weights(g)
         x_grouped = regroup_x("gpsimd", 1, True)
 
         column_bank_of = {}
@@ -416,8 +424,10 @@ def tile_pam_module_pa_kernel(tc, x, Wq, bq, Wk, bk, Wv, bv, out_0, out_1, out_2
                 while n_done < len(waiting) and waiting[n_done][0] <= step:
                     waiting[n_done][1](*waiting[n_done][2])
                     n_done += 1
+                if c == 0 and m + TRANSPOSES_AHEAD < O_TILES:
+                    transpose_weights(m + TRANSPOSES_AHEAD)
                 if c == 0 and m + WEIGHTS_AHEAD < O_TILES:
-                    prepare_weights(m + WEIGHTS_AHEAD)
+                    quantise_weights(m + WEIGHTS_AHEAD)
                 if (c, m) == (1, BIAS_TRANSPOSED_AT_TILE_OF_CHUNK_1):
                     transpose_bias()
                 if m in QUANTISE_AT_TILES and c + 1 < N_CHUNKS:

@@ -39,11 +39,11 @@ GPSIMD_COLUMNS_TILE = 0
 LAG = 4
 
 WEIGHTS_AHEAD = 2
-X_LOADS_FOLLOW_WEIGHT_TILES = (5, 9)
+X_LOADS_FOLLOW_WEIGHT_TILES = {1: (0, 1), 5: (1, 0), 9: (1, 1)}
 QUANTISE_AT_TILES = (5, 7)
 SCALAR_REGROUPS_AT_TILES = (8, 0, 2, 4)
 
-WARM_MATMULS_BEFORE_LOADS_LAND = 9
+WARM_MATMULS_BEFORE_LOADS_LAND = 6
 BIAS_TRANSPOSED_AT_TILE_OF_CHUNK_1 = 4
 TRANSPOSES_AHEAD = 4
 
@@ -112,12 +112,11 @@ def tile_pam_module_pa_kernel(tc, x, Wq, bq, Wk, bk, Wv, bv, out_0, out_1, out_2
                 in_=x_passes[n, g][:, :, CHUNK * part : CHUNK * (part + 1)],
             )
 
-        for g in range(PASSES):
-            load_x(0, g)
+        load_x(0, 0)
         for m in range(O_TILES):
             nc.sync.dma_start(out=w_raw_tiles[m][:], in_=weight_rows[m])
             if m in X_LOADS_FOLLOW_WEIGHT_TILES:
-                load_x(1, X_LOADS_FOLLOW_WEIGHT_TILES.index(m))
+                load_x(*X_LOADS_FOLLOW_WEIGHT_TILES[m])
         for c in range(2, N_CHUNKS):
             for g in range(PASSES):
                 load_x(c, g)
@@ -404,12 +403,16 @@ def tile_pam_module_pa_kernel(tc, x, Wq, bq, Wk, bk, Wv, bv, out_0, out_1, out_2
                 in_=pooled[:, n_alone:GROUP, :],
             )
 
-        x_grouped = regroup_x("vector", 0, True)
+        x_grouped = x_grouped_pool.tile(
+            [P, PASSES, HALVES, HALF_CHUNK, PACK], BF16, align_bytes=64
+        )
         x_mx = new_x_mx()
         assert WEIGHTS_AHEAD == PASSES
         for m in range(TRANSPOSES_AHEAD):
             transpose_weights(m)
         for g in range(PASSES):
+            for h in range(HALVES):
+                regroup_piece("vector", x_grouped, 0, g, h)
             quantise_x_pass(x_grouped, x_mx, g)
             quantise_weights(g)
         x_grouped = regroup_x("gpsimd", 1, True)

from contextlib import ExitStack

import concourse.mybir as mybir
from concourse.masks import make_identity

F32 = mybir.dt.float32
BF16 = mybir.dt.bfloat16
U32 = mybir.dt.uint32
U8 = mybir.dt.uint8
FP8X4 = mybir.dt.float8_e4m3fn_x4
ADD = mybir.AluOpType.add
MULT = mybir.AluOpType.mult
AXIS_X = mybir.AxisListType.X
AXIS_XY = mybir.AxisListType.XY
COPY = mybir.ActivationFunctionType.Copy

P = 128
PACK = 4
K_PASS = P * PACK
IMAGES, CHANNELS, HEIGHT, WIDTH = 2, 1024, 32, 64
PASSES = CHANNELS // K_PASS
O_TILES = 10
CHUNK = 512
CHUNK_ROWS = CHUNK // WIDTH
IMAGE_CHUNKS = HEIGHT // CHUNK_ROWS
N_CHUNKS = IMAGES * IMAGE_CHUNKS
HALVES = 2
HALF_WIDTH = WIDTH // HALVES
HALF_CHUNK = CHUNK // HALVES
PSUM_BANKS = 8

GROUP = 5
MULTIPLIED_TWICE = (1, 5, 7)

SCALAR_ROWS_TILES = (0, 2, 4, 6, 8, 9)
ALTERNATING_TILE = 9
FIRST_SCALAR_ROWS_TILE_OF_CHUNK_0 = 2
GPSIMD_COLUMNS_TILE = 0
LAG = 4

WEIGHTS_AHEAD = 2
X_LOADS_FOLLOW_WEIGHT_TILES = {1: (0, 1), 5: (1, 0), 9: (1, 1)}
QUANTISE_AT_TILES = (5, 7)
SCALAR_REGROUPS_AT_TILES = (8, 0, 2, 4)

WARM_MATMULS_BEFORE_LOADS_LAND = 6
BIAS_TRANSPOSED_AT_TILE_OF_CHUNK_1 = 4
TRANSPOSES_AHEAD = 4

FLOPS = 2 * O_TILES * P * CHANNELS * IMAGES * HEIGHT * WIDTH


def tile_pam_module_pa_kernel(tc, x, Wq, bq, Wk, bk, Wv, bv, out_0, out_1, out_2):
    nc = tc.nc
    n_multiplied_twice = len(MULTIPLIED_TWICE)

    x_passes = x.rearrange("n (g p t) h w -> n g p t (h w)", g=PASSES, p=P, t=PACK)
    weight_rows = [Wq, Wk] + [Wv[P * r : P * (r + 1), :] for r in range(O_TILES - 2)]
    out_rows = [out_0, out_1] + [out_2[:, P * r : P * (r + 1), :] for r in range(O_TILES - 2)]

    with ExitStack() as stack:
        stack.enter_context(tc.manual_schedule())
        const = stack.enter_context(tc.tile_pool(name="const", bufs=1))
        x_raw_pool = stack.enter_context(tc.tile_pool(name="x_raw", bufs=N_CHUNKS))
        w_raw_pool = stack.enter_context(tc.tile_pool(name="w_raw", bufs=O_TILES))
        x_grouped_pool = stack.enter_context(tc.tile_pool(name="x_grouped", bufs=1))
        w_grouped_pool = stack.enter_context(tc.tile_pool(name="w_grouped", bufs=TRANSPOSES_AHEAD))
        x_mx_pool = stack.enter_context(tc.tile_pool(name="x_mx", bufs=2))
        copy_pool = stack.enter_context(tc.tile_pool(name="copy", bufs=2 * LAG))
        tree_pool = stack.enter_context(tc.tile_pool(name="tree", bufs=2))
        result_pool = stack.enter_context(tc.tile_pool(name="result", bufs=2))
        column_banks = stack.enter_context(
            tc.psum_pool(name="column_banks", bufs=n_multiplied_twice)
        )
        banks = stack.enter_context(
            tc.psum_pool(name="banks", bufs=PSUM_BANKS - n_multiplied_twice)
        )

        warm_in = const.tile([P, 1], F32)
        nc.vector.memset(warm_in[:], 0.0)
        warm_out = const.tile([P, 1], F32)
        nc.scalar.activation(out=warm_out[:], in_=warm_in[:], func=COPY)

        warm_operand = const.tile([P, CHUNK], BF16)
        nc.gpsimd.memset(warm_operand[:], 0.0)
        warm_bank = banks.tile([P, CHUNK], F32, tag="bank")

        def warm_tensor_engine(n_matmuls):
            for k in range(n_matmuls):
                nc.tensor.matmul(
                    warm_bank[:], lhsT=warm_operand[:, 0:P], rhs=warm_operand[:], start=True, stop=True
                )

        warm_tensor_engine(WARM_MATMULS_BEFORE_LOADS_LAND)

        identity = const.tile([P, P], F32)
        make_identity(nc, identity[:])

        x_raw_tiles = []
        for c in range(N_CHUNKS):
            x_raw = x_raw_pool.tile([P, PASSES, PACK, CHUNK], BF16)
            x_raw_tiles.append(x_raw)
        w_raw_tiles = []
        for m in range(O_TILES):
            w_raw = w_raw_pool.tile([P, CHANNELS], BF16)
            w_raw_tiles.append(w_raw)

        def load_x(c, g):
            n, part = divmod(c, IMAGE_CHUNKS)
            nc.sync.dma_start(
                out=x_raw_tiles[c][:, g],
                in_=x_passes[n, g][:, :, CHUNK * part : CHUNK * (part + 1)],
            )

        load_x(0, 0)
        for m in range(O_TILES):
            nc.sync.dma_start(out=w_raw_tiles[m][:], in_=weight_rows[m])
            if m in X_LOADS_FOLLOW_WEIGHT_TILES:
                load_x(*X_LOADS_FOLLOW_WEIGHT_TILES[m])
        for c in range(2, N_CHUNKS):
            for g in range(PASSES):
                load_x(c, g)

        bias_rows = const.tile([P, P], BF16)
        nc.vector.memset(bias_rows[:], 0.0)
        nc.scalar.dma_start(out=bias_rows[0:1, :], in_=bq.rearrange("(r o) -> r o", r=1))
        nc.scalar.dma_start(out=bias_rows[1:2, :], in_=bk.rearrange("(r o) -> r o", r=1))
        nc.scalar.dma_start(
            out=bias_rows[2:O_TILES, :], in_=bv.rearrange("(r o) -> r o", r=O_TILES - 2)
        )

        w_words = const.tile([P, O_TILES, PASSES * P], U32, align_bytes=64)
        w_scales = const.tile([P, O_TILES, PASSES * P], U8, align_bytes=64)
        bias = const.tile([P, O_TILES], F32)
        bias_wide = const.tile([P, O_TILES, WIDTH], F32)
        row_sums = const.tile([P, IMAGES, O_TILES, HEIGHT], F32)
        column_parts = const.tile([P, IMAGES, IMAGE_CHUNKS, O_TILES, WIDTH], F32)
        for m in MULTIPLIED_TWICE:
            nc.gpsimd.memset(column_parts[:, :, 0 : IMAGE_CHUNKS - 1, m, :], 0.0)
        earlier_parts = const.tile([P, IMAGES, O_TILES, WIDTH], F32)

        w_grouped_of = {}

        def transpose_weights(m):
            words = w_raw_tiles[m][:].bitcast(F32)
            pairs = K_PASS // 2
            transposed = banks.tile([P, PASSES * 2, P], F32, tag="bank")
            for g in range(PASSES):
                for u in range(2):
                    nc.tensor.transpose(
                        transposed[:, 2 * g + u, :],
                        words[:, pairs * g + u : pairs * (g + 1) : 2],
                        identity[:],
                    )
            w_grouped = w_grouped_pool.tile([P, PASSES * P * PACK], BF16, align_bytes=64)
            nc.scalar.copy(
                out=w_grouped[:].bitcast(F32).rearrange("p (g o u) -> p g o u", g=PASSES, u=2),
                in_=transposed[:].rearrange("p (g u) o -> p g o u", u=2),
            )
            w_grouped_of[m] = w_grouped

        def quantise_weights(m):
            nc.vector.quantize_mx(
                out=w_words[:, m, :].bitcast(FP8X4),
                scales=w_scales[:, m, :],
                in_=w_grouped_of[m][:],
            )

        bias_rows_f32 = const.tile([P, P], F32)

        def cast_bias():
            nc.vector.tensor_copy(out=bias_rows_f32[:], in_=bias_rows[:])

        def transpose_bias():
            bias_columns = banks.tile([P, P], F32, tag="bank")
            nc.tensor.transpose(bias_columns[:], bias_rows_f32[:], identity[:])
            nc.vector.tensor_copy(out=bias[:], in_=bias_columns[:, 0:O_TILES])
            nc.gpsimd.tensor_scalar(
                out=bias_wide[:],
                in0=bias[:].unsqueeze(2).to_broadcast([P, O_TILES, WIDTH]),
                scalar1=1.0,
                scalar2=0.0,
                op0=MULT,
                op1=ADD,
            )

        def regroup_piece(engine, x_grouped, c, g, h, rows=slice(0, CHUNK_ROWS)):
            out = x_grouped[:, g, h].rearrange("p (i j) t -> p i j t", j=HALF_WIDTH)[:, rows]
            in_ = x_raw_tiles[c][:, g].rearrange(
                "p t (i h j) -> p h i j t", h=HALVES, j=HALF_WIDTH
            )[:, h, rows]
            if engine == "scalar":
                nc.scalar.copy(out=out, in_=in_)
            elif engine == "vector":
                nc.vector.tensor_copy(out=out, in_=in_)
            else:
                nc.gpsimd.tensor_scalar(
                    out=out, in0=in_, scalar1=1.0, scalar2=0.0, op0=MULT, op1=ADD
                )

        def regroup_x(engine, c, last_piece_too):
            x_grouped = x_grouped_pool.tile(
                [P, PASSES, HALVES, HALF_CHUNK, PACK], BF16, align_bytes=64
            )
            for g in range(PASSES):
                for h in range(HALVES):
                    if last_piece_too or (g, h) != (PASSES - 1, HALVES - 1):
                        regroup_piece(engine, x_grouped, c, g, h)
            return x_grouped

        def new_x_mx():
            x_words = x_mx_pool.tile([P, PASSES, CHUNK], U32, align_bytes=64)
            x_scales = x_mx_pool.tile([P, PASSES, CHUNK], U8, align_bytes=64)
            return x_words, x_scales

        def quantise_x_pass(x_grouped, x_mx, g):
            x_words, x_scales = x_mx
            nc.vector.quantize_mx(
                out=x_words[:, g, :].bitcast(FP8X4),
                scales=x_scales[:, g, :],
                in_=x_grouped[:, g].rearrange("p h w t -> p (h w t)"),
            )

        def multiply(out, m, g, x_mx, columns, start, stop):
            x_words, x_scales = x_mx
            nc.tensor.matmul_mx(
                out=out,
                lhsT=w_words[:, m, P * g : P * (g + 1)].bitcast(FP8X4),
                lhsT_scale=w_scales[:, m, P * g : P * (g + 1)],
                rhs=x_words[:, g, columns].bitcast(FP8X4),
                rhs_scale=x_scales[:, g, columns],
                start=start,
                stop=stop,
            )

        def sum_down_columns(out, bank):
            nc.vector.tensor_reduce(
                out=out.rearrange("p (h j) -> p h j", h=HALVES),
                in_=bank.rearrange("p (h i j) -> p h j i", h=HALVES, j=HALF_WIDTH),
                axis=AXIS_X,
                op=ADD,
            )

        def gpsimd_sum_down_columns(out, product_copy):
            rows = product_copy.rearrange("p (h i j) -> p h i j", h=HALVES, j=HALF_WIDTH)
            four = tree_pool.tile([P, HALVES, CHUNK_ROWS // 2, HALF_WIDTH], F32)
            nc.gpsimd.tensor_tensor(
                out=four[:], in0=rows[:, :, 0:4, :], in1=rows[:, :, 4:8, :], op=ADD
            )
            two = tree_pool.tile([P, HALVES, CHUNK_ROWS // 4, HALF_WIDTH], F32)
            nc.gpsimd.tensor_tensor(
                out=two[:], in0=four[:, :, 0:2, :], in1=four[:, :, 2:4, :], op=ADD
            )
            nc.gpsimd.tensor_tensor(
                out=out.rearrange("p (h j) -> p h j", h=HALVES),
                in0=two[:, :, 0, :],
                in1=two[:, :, 1, :],
                op=ADD,
            )

        def whole_product(m, x_mx):
            product = banks.tile([P, CHUNK], F32, tag="bank")
            for g in range(PASSES):
                multiply(product[:], m, g, x_mx, slice(0, CHUNK), g == 0, g == PASSES - 1)
            return product

        def scalar_rows_tile(n, part, m, x_mx, vector_sums_columns):
            product = whole_product(m, x_mx)
            if vector_sums_columns:
                sum_down_columns(column_parts[:, n, part, m, :], product[:])
            product_copy = copy_pool.tile([P, CHUNK], F32)
            product_rows = product[:].rearrange("p (h i j) -> p i h j", h=HALVES, j=HALF_WIDTH)
            copy_rows = product_copy[:].rearrange("p (h i j) -> p i h j", h=HALVES, j=HALF_WIDTH)
            for i in range(CHUNK_ROWS):
                row = CHUNK_ROWS * part + i
                nc.scalar.activation(
                    out=copy_rows[:, i],
                    in_=product_rows[:, i],
                    func=COPY,
                    accum_out=row_sums[:, n, m, row : row + 1],
                )
            return product_copy

        def vector_tile(n, part, m, x_mx):
            product = whole_product(m, x_mx)
            sum_down_columns(column_parts[:, n, part, m, :], product[:])
            nc.vector.tensor_reduce(
                out=row_sums[:, n, m, CHUNK_ROWS * part : CHUNK_ROWS * (part + 1)],
                in_=product[:].rearrange("p (h i j) -> p i h j", h=HALVES, j=HALF_WIDTH),
                axis=AXIS_XY,
                op=ADD,
            )

        def multiplied_twice_tile(n, part, m, x_mx, column_bank):
            row_part = banks.tile([P, HALF_CHUNK], F32, tag="bank")
            for g in range(PASSES):
                for h in range(HALVES):
                    multiply(
                        row_part[:],
                        m,
                        g,
                        x_mx,
                        slice(HALF_CHUNK * h, HALF_CHUNK * (h + 1)),
                        g == 0 and h == 0,
                        g == PASSES - 1 and h == HALVES - 1,
                    )
            nc.vector.tensor_reduce(
                out=row_sums[:, n, m, CHUNK_ROWS * part : CHUNK_ROWS * (part + 1)],
                in_=row_part[:].rearrange("p (i j) -> p i j", j=HALF_WIDTH),
                axis=AXIS_X,
                op=ADD,
            )
            for g in range(PASSES):
                multiply(
                    column_bank[:],
                    m,
                    g,
                    x_mx,
                    slice(0, CHUNK),
                    part == 0 and g == 0,
                    part == IMAGE_CHUNKS - 1 and g == PASSES - 1,
                )
            if part == IMAGE_CHUNKS - 1:
                sum_down_columns(column_parts[:, n, part, m, :], column_bank[:])

        def add_earlier_parts(n, first):
            group = slice(first, first + GROUP)
            nc.gpsimd.tensor_tensor(
                out=earlier_parts[:, n, group],
                in0=column_parts[:, n, 0, group],
                in1=column_parts[:, n, 1, group],
                op=ADD,
            )
            for part in range(2, IMAGE_CHUNKS - 1):
                nc.gpsimd.tensor_tensor(
                    out=earlier_parts[:, n, group],
                    in0=earlier_parts[:, n, group],
                    in1=column_parts[:, n, part, group],
                    op=ADD,
                )
            nc.gpsimd.tensor_scalar(
                out=earlier_parts[:, n, group],
                in0=earlier_parts[:, n, group],
                scalar1=1.0 / HEIGHT,
                scalar2=0.0,
                op0=MULT,
                op1=ADD,
            )
            nc.gpsimd.tensor_tensor(
                out=earlier_parts[:, n, group],
                in0=earlier_parts[:, n, group],
                in1=bias_wide[:, group],
                op=ADD,
            )

        def finish(n, first):
            group = slice(first, first + GROUP)
            pooled = result_pool.tile([P, GROUP, HEIGHT + WIDTH], F32)
            if (n, first) == (IMAGES - 1, 0):
                for out, in0, factor, in1 in (
                    (
                        pooled[:, :, 0:HEIGHT],
                        row_sums[:, n, group],
                        1.0 / WIDTH,
                        bias_wide[:, group, 0:HEIGHT],
                    ),
                    (
                        pooled[:, :, HEIGHT:],
                        column_parts[:, n, IMAGE_CHUNKS - 1, group],
                        1.0 / HEIGHT,
                        earlier_parts[:, n, group],
                    ),
                ):
                    nc.gpsimd.tensor_scalar(
                        out=out, in0=in0, scalar1=factor, scalar2=0.0, op0=MULT, op1=ADD
                    )
                    nc.gpsimd.tensor_tensor(out=out, in0=out, in1=in1, op=ADD)
            else:
                nc.vector.scalar_tensor_tensor(
                    out=pooled[:, :, 0:HEIGHT],
                    in0=row_sums[:, n, group],
                    scalar=1.0 / WIDTH,
                    in1=bias[:, group].unsqueeze(2).to_broadcast([P, GROUP, HEIGHT]),
                    op0=MULT,
                    op1=ADD,
                )
                nc.vector.scalar_tensor_tensor(
                    out=pooled[:, :, HEIGHT:],
                    in0=column_parts[:, n, IMAGE_CHUNKS - 1, group],
                    scalar=1.0 / HEIGHT,
                    in1=earlier_parts[:, n, group],
                    op0=MULT,
                    op1=ADD,
                )
            n_alone = max(0, 2 - first)
            for k in range(n_alone):
                nc.sync.dma_start(out=out_rows[first + k][n], in_=pooled[:, k, :])
            v_first = first + n_alone - 2
            nc.sync.dma_start(
                out=out_2[n, P * v_first : P * (first + GROUP - 2), :].rearrange(
                    "(k p) f -> p k f", p=P
                ),
                in_=pooled[:, n_alone:GROUP, :],
            )

        x_grouped = x_grouped_pool.tile(
            [P, PASSES, HALVES, HALF_CHUNK, PACK], BF16, align_bytes=64
        )
        x_mx = new_x_mx()
        assert WEIGHTS_AHEAD == PASSES
        for m in range(TRANSPOSES_AHEAD):
            transpose_weights(m)
        for g in range(PASSES):
            for h in range(HALVES):
                regroup_piece("vector", x_grouped, 0, g, h)
            quantise_x_pass(x_grouped, x_mx, g)
            quantise_weights(g)
        x_grouped = regroup_x("gpsimd", 1, True)

        column_bank_of = {}
        waiting = []
        n_done = 0
        for c in range(N_CHUNKS):
            n, part = divmod(c, IMAGE_CHUNKS)
            for m in range(O_TILES):
                step = O_TILES * c + m
                while n_done < len(waiting) and waiting[n_done][0] <= step:
                    waiting[n_done][1](*waiting[n_done][2])
                    n_done += 1
                if c == 0 and m + TRANSPOSES_AHEAD < O_TILES:
                    transpose_weights(m + TRANSPOSES_AHEAD)
                if c == 0 and m + WEIGHTS_AHEAD < O_TILES:
                    quantise_weights(m + WEIGHTS_AHEAD)
                if (c, m) == (1, BIAS_TRANSPOSED_AT_TILE_OF_CHUNK_1):
                    transpose_bias()
                if m in QUANTISE_AT_TILES and c + 1 < N_CHUNKS:
                    g = QUANTISE_AT_TILES.index(m)
                    if g == 0:
                        next_x_mx = new_x_mx()
                    quantise_x_pass(x_grouped, next_x_mx, g)
                    if g == PASSES - 1 and c + 2 < N_CHUNKS:
                        x_grouped = regroup_x("gpsimd", c + 2, False)
                if m in SCALAR_REGROUPS_AT_TILES:
                    k = SCALAR_REGROUPS_AT_TILES.index(m)
                    chunk = c + 2 if k == 0 else c + 1
                    if 2 <= chunk < N_CHUNKS:
                        share = CHUNK_ROWS // len(SCALAR_REGROUPS_AT_TILES)
                        regroup_piece(
                            "scalar",
                            x_grouped,
                            chunk,
                            PASSES - 1,
                            HALVES - 1,
                            slice(share * k, share * (k + 1)),
                        )
                if m in MULTIPLIED_TWICE:
                    if part == 0:
                        column_bank = column_banks.tile([P, CHUNK], F32)
                        column_bank_of[m] = column_bank
                    multiplied_twice_tile(n, part, m, x_mx, column_bank_of[m])
                elif (
                    m not in SCALAR_ROWS_TILES
                    or (m == ALTERNATING_TILE and c % 2 == 1)
                    or (c == 0 and m < FIRST_SCALAR_ROWS_TILE_OF_CHUNK_0)
                ):
                    vector_tile(n, part, m, x_mx)
                else:
                    scalar_rows_tile(n, part, m, x_mx, True)
                if part == IMAGE_CHUNKS - 2 and (m + 1) % GROUP == 0:
                    waiting.append((step + LAG, add_earlier_parts, (n, m + 1 - GROUP)))
                if part == IMAGE_CHUNKS - 1 and (m + 1) % GROUP == 0:
                    waiting.append((step + LAG, finish, (n, m + 1 - GROUP)))
            if c == 0:
                cast_bias()
            if c + 1 < N_CHUNKS:
                x_mx = next_x_mx
        while n_done < len(waiting):
            waiting[n_done][1](*waiting[n_done][2])
            n_done += 1
